import numpy as np
import ml_dtypes


def mxq(x, axis, fmt="e4m3"):
    dtype, down = {"e4m3": (ml_dtypes.float8_e4m3fn, 7), "e5m2": (ml_dtypes.float8_e5m2, 14)}[fmt]
    v = np.moveaxis(np.asarray(x, np.float32).astype(ml_dtypes.bfloat16).astype(np.float64), axis, -1)
    blocks = v.reshape(v.shape[:-1] + (-1, 32))
    amax = np.abs(blocks).max(-1, keepdims=True)
    byte = np.maximum(np.where(amax > 0, np.frexp(amax)[1] - 1 + 127, 0) - down, 1)
    scale = np.exp2(byte - 127.0)
    codes = (blocks / scale).astype(np.float32).astype(dtype).astype(np.float64)
    return np.moveaxis((codes * scale).reshape(v.shape), -1, axis)


WIDE = False


def mx_kscale(k):
    if not WIDE:
        return np.ones(k)
    levels = np.array([10, -10, 5, -5, 0])
    a = np.random.permutation(np.resize(levels, k // 512 * 4)).reshape(k // 512, 4)
    idx = np.arange(k)
    return np.exp2(a[idx // 512, idx % 128 // 32])


BF16 = ml_dtypes.bfloat16


def bf(x):
    return np.asarray(x, np.float32).astype(BF16)


def f64(x):
    return np.asarray(x).astype(np.float64)


B, X, N, OS = 256, 16384, 768, 256
H = N - OS


def setup_inputs():
    s, t = mx_kscale(X), mx_kscale(H)
    std0 = np.sqrt(2.0 / X)
    std1 = np.sqrt(2.0 / (X + H))
    row_scale = np.concatenate([std0 * t, np.full(OS, std1)])
    bias_scale = np.concatenate([t, np.ones(OS)])
    return {"x": bf(np.random.standard_normal((B, X)) * s),
            "w0": bf(np.random.standard_normal((N, X)) * row_scale[:, None] / s),
            "w1": bf(np.random.standard_normal((OS, H)) * std1 / t),
            "biases": bf(np.random.random(N) * bias_scale)}


def reference(x, w0, w1, biases):
    n = w0.shape[0]
    os_ = w1.shape[0]
    z = (mxq(f64(x), 1, "e4m3") @ mxq(f64(w0), 1, "e4m3").T) + f64(biases)
    h = np.maximum(z[:, : n - os_], 0.0)
    return z[:, n - os_:] + (mxq(h, 1, "e4m3") @ mxq(f64(w1), 1, "e4m3").T)

@@ -1,0 +1,224 @@
+from contextlib import ExitStack
+
+import concourse.mybir as mybir
+from concourse.masks import make_identity
+
+F32 = mybir.dt.float32
+BF16 = mybir.dt.bfloat16
+U32 = mybir.dt.uint32
+U8 = mybir.dt.uint8
+FP8X4 = mybir.dt.float8_e4m3fn_x4
+ACT = mybir.ActivationFunctionType
+
+P = 128
+PACK = 4
+K_PASS = P * PACK
+
+BATCH = 256
+FEATURES = 16384
+NODES = 768
+HIDDEN = 512
+OUTPUTS = NODES - HIDDEN
+
+BATCH_BLOCKS = BATCH // P
+NODE_BLOCKS = NODES // P
+HIDDEN_BLOCKS = HIDDEN // P
+OUTPUT_BLOCKS = OUTPUTS // P
+
+PASSES = FEATURES // K_PASS
+CHUNK = 4096
+CHUNKS = FEATURES // CHUNK
+CHUNK_PASSES = CHUNK // K_PASS
+BANK_PASSES = 2
+CHUNK_BANKS = CHUNK_PASSES // BANK_PASSES
+VECTOR_BANK = 2
+QUANT_COLS = 2048
+RAW_BUFS = 10
+
+FLOPS = 2 * BATCH * FEATURES * NODES + 2 * BATCH * HIDDEN * OUTPUTS
+
+
+def flip_chunk(nc, banks, identity, raw, grouped_words):
+    raw_words = raw[:].bitcast(F32)
+    for bank in range(CHUNK_BANKS):
+        flipped = banks.tile([P, BANK_PASSES, 2, P], F32, tag="flipped")
+        for g in range(BANK_PASSES):
+            for u in range(2):
+                first = ((bank * BANK_PASSES + g) * 2 + u) * P
+                nc.tensor.transpose(
+                    flipped[:, g, u, :], raw_words[:, first : first + P], identity[:]
+                )
+        dest = grouped_words[:, bank * BANK_PASSES : (bank + 1) * BANK_PASSES, :, :]
+        source = flipped[:].rearrange("p g u r -> p g r u")
+        if bank == VECTOR_BANK:
+            nc.vector.tensor_copy(out=dest, in_=source)
+        else:
+            nc.scalar.copy(out=dest, in_=source)
+
+
+def quantise(nc, grouped, codes, scales):
+    total = grouped.shape[1]
+    width = min(QUANT_COLS, total)
+    for first in range(0, total, width):
+        words = slice(first // PACK, (first + width) // PACK)
+        nc.vector.quantize_mx(
+            out=codes[:, words].bitcast(FP8X4),
+            scales=scales[:, words],
+            in_=grouped[:, first : first + width],
+        )
+
+
+def tile_spn_k_kernel(tc, x, w0, w1, biases, out):
+    nc = tc.nc
+    with ExitStack() as ctx:
+        ctx.enter_context(tc.manual_schedule())
+        consts = ctx.enter_context(tc.tile_pool(name="consts", bufs=1))
+        raws = ctx.enter_context(tc.tile_pool(name="raws", bufs=RAW_BUFS))
+        stage = ctx.enter_context(tc.tile_pool(name="stage", bufs=3))
+        banks = ctx.enter_context(tc.psum_pool(name="banks", bufs=4))
+        sums = ctx.enter_context(tc.psum_pool(name="sums", bufs=4))
+
+        bias_rows = consts.tile([P, P], BF16)
+        nc.vector.memset(bias_rows[:], 0.0)
+        ident_f32 = consts.tile([P, P], F32)
+        make_identity(nc, ident_f32[:])
+        ident_bf16 = consts.tile([P, P], BF16)
+        make_identity(nc, ident_bf16[:])
+
+        nc.sync.dma_start(
+            out=bias_rows[0:NODE_BLOCKS, :], in_=biases.rearrange("(n p) -> n p", p=P)
+        )
+        w1_raw = consts.tile([P, OUTPUT_BLOCKS, HIDDEN], BF16)
+        nc.sync.dma_start(out=w1_raw[:], in_=w1.rearrange("(j p) h -> p j h", p=P))
+
+        bias_flipped = banks.tile([P, P], BF16, tag="flipped")
+        nc.tensor.transpose(bias_flipped[:], bias_rows[:], ident_bf16[:])
+        bias_cols = consts.tile([P, NODE_BLOCKS], F32)
+        nc.vector.tensor_copy(out=bias_cols[:], in_=bias_flipped[:, 0:NODE_BLOCKS])
+
+        w1_flipped = banks.tile([P, OUTPUT_BLOCKS, PACK, P], BF16, tag="flipped")
+        for j in range(OUTPUT_BLOCKS):
+            for t in range(PACK):
+                nc.tensor.transpose(
+                    w1_flipped[:, j, t, :], w1_raw[:, j, t * P : (t + 1) * P], ident_bf16[:]
+                )
+        w1_grouped = consts.tile([P, OUTPUT_BLOCKS, P, PACK], BF16, align_bytes=64)
+        nc.vector.tensor_copy(
+            out=w1_grouped[:], in_=w1_flipped[:].rearrange("p j t o -> p j o t")
+        )
+        w1_codes = consts.tile([P, OUTPUTS], U32, align_bytes=64)
+        w1_scales = consts.tile([P, OUTPUTS], U8, align_bytes=64)
+        quantise(nc, w1_grouped[:].rearrange("p j o t -> p (j o t)"), w1_codes, w1_scales)
+
+        x_codes = consts.tile([P, PASSES * BATCH], U32, align_bytes=64)
+        x_scales = consts.tile([P, PASSES * BATCH], U8, align_bytes=64)
+        h_planes = consts.tile([P, PACK, BATCH], BF16)
+        h_grouped = consts.tile([P, BATCH, PACK], BF16, align_bytes=64)
+        h_codes = consts.tile([P, BATCH], U32, align_bytes=64)
+        h_scales = consts.tile([P, BATCH], U8, align_bytes=64)
+        z_out = consts.tile([P, OUTPUT_BLOCKS, BATCH], F32)
+
+        def load(rows, c):
+            raw = raws.tile([P, CHUNK], BF16)
+            nc.sync.dma_start(out=raw[:], in_=rows[:, c * CHUNK : (c + 1) * CHUNK])
+            return raw
+
+        def stage_x(c):
+            x_grouped = stage.tile([P, BATCH_BLOCKS * CHUNK], BF16, align_bytes=64, bufs=2)
+            x_words = x_grouped[:].bitcast(F32).rearrange(
+                "p (g b r u) -> p g b r u", b=BATCH_BLOCKS, r=P, u=2
+            )
+            for b in range(BATCH_BLOCKS):
+                raw = load(x[b * P : (b + 1) * P, :], c)
+                flip_chunk(nc, banks, ident_f32, raw, x_words[:, :, b, :, :])
+            cols = slice(c * CHUNK_PASSES * BATCH, (c + 1) * CHUNK_PASSES * BATCH)
+            quantise(nc, x_grouped, x_codes[:, cols], x_scales[:, cols])
+
+        def stage_nodes(n, c):
+            w_grouped = stage.tile([P, CHUNK], BF16, align_bytes=64)
+            w_words = w_grouped[:].bitcast(F32).rearrange("p (g r u) -> p g r u", r=P, u=2)
+            raw = load(w0[n * P : (n + 1) * P, :], c)
+            flip_chunk(nc, banks, ident_f32, raw, w_words)
+            w_codes = stage.tile([P, CHUNK_PASSES * P], U32, align_bytes=64)
+            w_scales = stage.tile([P, CHUNK_PASSES * P], U8, align_bytes=64)
+            quantise(nc, w_grouped, w_codes, w_scales)
+            return w_codes, w_scales
+
+        accs = {}
+
+        def multiply(n, c, w_codes, w_scales):
+            if c == 0:
+                acc = sums.tile([P, BATCH], F32)
+                accs[n] = acc
+            acc = accs[n]
+            is_hidden = n < HIDDEN_BLOCKS
+            for g in range(CHUNK_PASSES):
+                k_pass = c * CHUNK_PASSES + g
+                nc.tensor.matmul_mx(
+                    out=acc[:],
+                    lhsT=w_codes[:, g * P : (g + 1) * P].bitcast(FP8X4),
+                    lhsT_scale=w_scales[:, g * P : (g + 1) * P],
+                    rhs=x_codes[:, k_pass * BATCH : (k_pass + 1) * BATCH].bitcast(FP8X4),
+                    rhs_scale=x_scales[:, k_pass * BATCH : (k_pass + 1) * BATCH],
+                    start=(k_pass == 0),
+                    stop=(is_hidden and k_pass == PASSES - 1),
+                )
+            if c < CHUNKS - 1:
+                return
+            if is_hidden:
+                nc.scalar.activation(
+                    out=h_planes[:, n, :],
+                    in_=acc[:],
+                    func=ACT.Relu,
+                    bias=bias_cols[:, n : n + 1],
+                    scale=1.0,
+                )
+                if n == HIDDEN_BLOCKS - 1:
+                    nc.vector.tensor_copy(
+                        out=h_grouped[:], in_=h_planes[:].rearrange("p t b -> p b t")
+                    )
+                    quantise(nc, h_grouped[:].rearrange("p b t -> p (b t)"), h_codes, h_scales)
+            else:
+                j = n - HIDDEN_BLOCKS
+                nc.tensor.matmul_mx(
+                    out=acc[:],
+                    lhsT=w1_codes[:, j * P : (j + 1) * P].bitcast(FP8X4),
+                    lhsT_scale=w1_scales[:, j * P : (j + 1) * P],
+                    rhs=h_codes[:].bitcast(FP8X4),
+                    rhs_scale=h_scales[:],
+                    start=False,
+                    stop=True,
+                )
+                nc.scalar.activation(
+                    out=z_out[:, j, :],
+                    in_=acc[:],
+                    func=ACT.Identity,
+                    bias=bias_cols[:, n : n + 1],
+                    scale=1.0,
+                )
+
+        node_chunks = [(n, c) for c in range(CHUNKS) for n in range(HIDDEN_BLOCKS)]
+        node_chunks += [(n, c) for n in range(HIDDEN_BLOCKS, NODE_BLOCKS) for c in range(CHUNKS)]
+        previous = None
+        for n, c in node_chunks:
+            if n == 0:
+                stage_x(c)
+            current = (n, c) + stage_nodes(n, c)
+            if previous is not None:
+                multiply(*previous)
+            previous = current
+        multiply(*previous)
+
+        for b in range(BATCH_BLOCKS):
+            back = banks.tile([P, OUTPUTS], F32, tag="flipped")
+            for j in range(OUTPUT_BLOCKS):
+                nc.tensor.transpose(
+                    back[:, j * P : (j + 1) * P], z_out[:, j, b * P : (b + 1) * P], ident_f32[:]
+                )
+            result = stage.tile([P, OUTPUTS], F32, bufs=2)
+            if b == 0:
+                nc.vector.tensor_copy(out=result[:], in_=back[:])
+                nc.sync.dma_start(out=out[b * P : (b + 1) * P, :], in_=result[:])
+            else:
+                nc.scalar.copy(out=result[:], in_=back[:])
+                nc.scalar.dma_start(out=out[b * P : (b + 1) * P, :], in_=result[:])

@@ -9,6 +9,7 @@ U32 = mybir.dt.uint32
 U8 = mybir.dt.uint8
 FP8X4 = mybir.dt.float8_e4m3fn_x4
 ACT = mybir.ActivationFunctionType
+ALU = mybir.AluOpType
 
 P = 128
 PACK = 4
@@ -20,10 +21,9 @@ NODES = 768
 HIDDEN = 512
 OUTPUTS = NODES - HIDDEN
 
-BATCH_BLOCKS = BATCH // P
+PAIR = 2
 NODE_BLOCKS = NODES // P
 HIDDEN_BLOCKS = HIDDEN // P
-OUTPUT_BLOCKS = OUTPUTS // P
 
 PASSES = FEATURES // K_PASS
 CHUNK = 4096
@@ -33,15 +33,16 @@ BANK_PASSES = 2
 CHUNK_BANKS = CHUNK_PASSES // BANK_PASSES
 VECTOR_BANK = 2
 QUANT_COLS = 2048
-RAW_BUFS = 10
+RAW_BUFS = 8
+PSUM_BANKS = 8
 
 FLOPS = 2 * BATCH * FEATURES * NODES + 2 * BATCH * HIDDEN * OUTPUTS
 
 
-def flip_chunk(nc, banks, identity, raw, grouped_words):
+def flip_chunk(nc, psum, identity, raw, grouped_words):
     raw_words = raw[:].bitcast(F32)
     for bank in range(CHUNK_BANKS):
-        flipped = banks.tile([P, BANK_PASSES, 2, P], F32, tag="flipped")
+        flipped = psum.tile([P, BANK_PASSES, 2, P], F32, tag="bank")
         for g in range(BANK_PASSES):
             for u in range(2):
                 first = ((bank * BANK_PASSES + g) * 2 + u) * P
@@ -74,9 +75,8 @@ def tile_spn_k_kernel(tc, x, w0, w1, biases, out):
         ctx.enter_context(tc.manual_schedule())
         consts = ctx.enter_context(tc.tile_pool(name="consts", bufs=1))
         raws = ctx.enter_context(tc.tile_pool(name="raws", bufs=RAW_BUFS))
-        stage = ctx.enter_context(tc.tile_pool(name="stage", bufs=3))
-        banks = ctx.enter_context(tc.psum_pool(name="banks", bufs=4))
-        sums = ctx.enter_context(tc.psum_pool(name="sums", bufs=4))
+        stage = ctx.enter_context(tc.tile_pool(name="stage", bufs=2))
+        psum = ctx.enter_context(tc.psum_pool(name="psum", bufs=PSUM_BANKS))
 
         bias_rows = consts.tile([P, P], BF16)
         nc.vector.memset(bias_rows[:], 0.0)
@@ -88,21 +88,21 @@ def tile_spn_k_kernel(tc, x, w0, w1, biases, out):
         nc.sync.dma_start(
             out=bias_rows[0:NODE_BLOCKS, :], in_=biases.rearrange("(n p) -> n p", p=P)
         )
-        w1_raw = consts.tile([P, OUTPUT_BLOCKS, HIDDEN], BF16)
+        w1_raw = consts.tile([P, PAIR, HIDDEN], BF16)
         nc.sync.dma_start(out=w1_raw[:], in_=w1.rearrange("(j p) h -> p j h", p=P))
 
-        bias_flipped = banks.tile([P, P], BF16, tag="flipped")
+        bias_flipped = psum.tile([P, P], BF16, tag="bank")
         nc.tensor.transpose(bias_flipped[:], bias_rows[:], ident_bf16[:])
         bias_cols = consts.tile([P, NODE_BLOCKS], F32)
         nc.vector.tensor_copy(out=bias_cols[:], in_=bias_flipped[:, 0:NODE_BLOCKS])
 
-        w1_flipped = banks.tile([P, OUTPUT_BLOCKS, PACK, P], BF16, tag="flipped")
-        for j in range(OUTPUT_BLOCKS):
+        w1_flipped = psum.tile([P, PAIR, PACK, P], BF16, tag="bank")
+        for j in range(PAIR):
             for t in range(PACK):
                 nc.tensor.transpose(
                     w1_flipped[:, j, t, :], w1_raw[:, j, t * P : (t + 1) * P], ident_bf16[:]
                 )
-        w1_grouped = consts.tile([P, OUTPUT_BLOCKS, P, PACK], BF16, align_bytes=64)
+        w1_grouped = consts.tile([P, PAIR, P, PACK], BF16, align_bytes=64)
         nc.vector.tensor_copy(
             out=w1_grouped[:], in_=w1_flipped[:].rearrange("p j t o -> p j o t")
         )
@@ -116,109 +116,115 @@ def tile_spn_k_kernel(tc, x, w0, w1, biases, out):
         h_grouped = consts.tile([P, BATCH, PACK], BF16, align_bytes=64)
         h_codes = consts.tile([P, BATCH], U32, align_bytes=64)
         h_scales = consts.tile([P, BATCH], U8, align_bytes=64)
-        z_out = consts.tile([P, OUTPUT_BLOCKS, BATCH], F32)
+        out_bias = consts.tile([P, OUTPUTS], BF16)
 
         def load(rows, c):
             raw = raws.tile([P, CHUNK], BF16)
             nc.sync.dma_start(out=raw[:], in_=rows[:, c * CHUNK : (c + 1) * CHUNK])
             return raw
 
-        def stage_x(c):
-            x_grouped = stage.tile([P, BATCH_BLOCKS * CHUNK], BF16, align_bytes=64, bufs=2)
-            x_words = x_grouped[:].bitcast(F32).rearrange(
-                "p (g b r u) -> p g b r u", b=BATCH_BLOCKS, r=P, u=2
+        def stage_pair(rows, c, codes, scales):
+            pair_grouped = stage.tile([P, PAIR * CHUNK], BF16, align_bytes=64)
+            pair_words = pair_grouped[:].bitcast(F32).rearrange(
+                "p (g b r u) -> p g b r u", b=PAIR, r=P, u=2
             )
-            for b in range(BATCH_BLOCKS):
-                raw = load(x[b * P : (b + 1) * P, :], c)
-                flip_chunk(nc, banks, ident_f32, raw, x_words[:, :, b, :, :])
-            cols = slice(c * CHUNK_PASSES * BATCH, (c + 1) * CHUNK_PASSES * BATCH)
-            quantise(nc, x_grouped, x_codes[:, cols], x_scales[:, cols])
+            for b in range(PAIR):
+                raw = load(rows[b * P : (b + 1) * P, :], c)
+                flip_chunk(nc, psum, ident_f32, raw, pair_words[:, :, b, :, :])
+            quantise(nc, pair_grouped, codes, scales)
 
-        def stage_nodes(n, c):
-            w_grouped = stage.tile([P, CHUNK], BF16, align_bytes=64)
+        def stage_hidden(n, c):
+            w_grouped = stage.tile([P, CHUNK], BF16, align_bytes=64, bufs=3)
             w_words = w_grouped[:].bitcast(F32).rearrange("p (g r u) -> p g r u", r=P, u=2)
             raw = load(w0[n * P : (n + 1) * P, :], c)
-            flip_chunk(nc, banks, ident_f32, raw, w_words)
-            w_codes = stage.tile([P, CHUNK_PASSES * P], U32, align_bytes=64)
-            w_scales = stage.tile([P, CHUNK_PASSES * P], U8, align_bytes=64)
+            flip_chunk(nc, psum, ident_f32, raw, w_words)
+            w_codes = stage.tile([P, CHUNK_PASSES * P], U32, align_bytes=64, bufs=3)
+            w_scales = stage.tile([P, CHUNK_PASSES * P], U8, align_bytes=64, bufs=3)
             quantise(nc, w_grouped, w_codes, w_scales)
             return w_codes, w_scales
 
-        accs = {}
+        hidden_sums = {}
 
-        def multiply(n, c, w_codes, w_scales):
+        def multiply_hidden(n, c, w_codes, w_scales):
             if c == 0:
-                acc = sums.tile([P, BATCH], F32)
-                accs[n] = acc
-            acc = accs[n]
-            is_hidden = n < HIDDEN_BLOCKS
+                hidden_sum = psum.tile([P, BATCH], F32, tag="bank")
+                hidden_sums[n] = hidden_sum
             for g in range(CHUNK_PASSES):
                 k_pass = c * CHUNK_PASSES + g
                 nc.tensor.matmul_mx(
-                    out=acc[:],
+                    out=hidden_sums[n][:],
                     lhsT=w_codes[:, g * P : (g + 1) * P].bitcast(FP8X4),
                     lhsT_scale=w_scales[:, g * P : (g + 1) * P],
                     rhs=x_codes[:, k_pass * BATCH : (k_pass + 1) * BATCH].bitcast(FP8X4),
                     rhs_scale=x_scales[:, k_pass * BATCH : (k_pass + 1) * BATCH],
                     start=(k_pass == 0),
-                    stop=(is_hidden and k_pass == PASSES - 1),
+                    stop=(k_pass == PASSES - 1),
                 )
-            if c < CHUNKS - 1:
-                return
-            if is_hidden:
+            if c == CHUNKS - 1:
                 nc.scalar.activation(
                     out=h_planes[:, n, :],
-                    in_=acc[:],
+                    in_=hidden_sums[n][:],
                     func=ACT.Relu,
                     bias=bias_cols[:, n : n + 1],
                     scale=1.0,
                 )
-                if n == HIDDEN_BLOCKS - 1:
-                    nc.vector.tensor_copy(
-                        out=h_grouped[:], in_=h_planes[:].rearrange("p t b -> p b t")
+
+        out_sums = {}
+
+        def multiply_outputs(c, o_codes, o_scales):
+            for b in range(PAIR):
+                if c == 0:
+                    out_sum = psum.tile([P, OUTPUTS], F32, tag="bank")
+                    out_sums[b] = out_sum
+                for g in range(CHUNK_PASSES):
+                    first = (c * CHUNK_PASSES + g) * BATCH + b * P
+                    nc.tensor.matmul_mx(
+                        out=out_sums[b][:],
+                        lhsT=x_codes[:, first : first + P].bitcast(FP8X4),
+                        lhsT_scale=x_scales[:, first : first + P],
+                        rhs=o_codes[:, g * OUTPUTS : (g + 1) * OUTPUTS].bitcast(FP8X4),
+                        rhs_scale=o_scales[:, g * OUTPUTS : (g + 1) * OUTPUTS],
+                        start=(c == 0 and g == 0),
+                        stop=False,
                     )
-                    quantise(nc, h_grouped[:].rearrange("p b t -> p (b t)"), h_codes, h_scales)
-            else:
-                j = n - HIDDEN_BLOCKS
-                nc.tensor.matmul_mx(
-                    out=acc[:],
-                    lhsT=w1_codes[:, j * P : (j + 1) * P].bitcast(FP8X4),
-                    lhsT_scale=w1_scales[:, j * P : (j + 1) * P],
-                    rhs=h_codes[:].bitcast(FP8X4),
-                    rhs_scale=h_scales[:],
-                    start=False,
-                    stop=True,
-                )
-                nc.scalar.activation(
-                    out=z_out[:, j, :],
-                    in_=acc[:],
-                    func=ACT.Identity,
-                    bias=bias_cols[:, n : n + 1],
-                    scale=1.0,
-                )
+                if c == CHUNKS - 1:
+                    nc.tensor.matmul_mx(
+                        out=out_sums[b][:],
+                        lhsT=h_codes[:, b * P : (b + 1) * P].bitcast(FP8X4),
+                        lhsT_scale=h_scales[:, b * P : (b + 1) * P],
+                        rhs=w1_codes[:].bitcast(FP8X4),
+                        rhs_scale=w1_scales[:],
+                        start=False,
+                        stop=True,
+                    )
+                    result = stage.tile([P, OUTPUTS], F32)
+                    nc.vector.tensor_tensor(
+                        out=result[:], in0=out_sums[b][:], in1=out_bias[:], op=ALU.add
+                    )
+                    nc.sync.dma_start(out=out[b * P : (b + 1) * P, :], in_=result[:])
 
-        node_chunks = [(n, c) for c in range(CHUNKS) for n in range(HIDDEN_BLOCKS)]
-        node_chunks += [(n, c) for n in range(HIDDEN_BLOCKS, NODE_BLOCKS) for c in range(CHUNKS)]
         previous = None
-        for n, c in node_chunks:
-            if n == 0:
-                stage_x(c)
-            current = (n, c) + stage_nodes(n, c)
-            if previous is not None:
-                multiply(*previous)
-            previous = current
-        multiply(*previous)
+        for c in range(CHUNKS):
+            cols = slice(c * CHUNK_PASSES * BATCH, (c + 1) * CHUNK_PASSES * BATCH)
+            stage_pair(x, c, x_codes[:, cols], x_scales[:, cols])
+            for n in range(HIDDEN_BLOCKS):
+                current = (n, c) + stage_hidden(n, c)
+                if previous is not None:
+                    multiply_hidden(*previous)
+                previous = current
 
-        for b in range(BATCH_BLOCKS):
-            back = banks.tile([P, OUTPUTS], F32, tag="flipped")
-            for j in range(OUTPUT_BLOCKS):
-                nc.tensor.transpose(
-                    back[:, j * P : (j + 1) * P], z_out[:, j, b * P : (b + 1) * P], ident_f32[:]
+        nc.sync.dma_start(out=out_bias[:], in_=biases[HIDDEN:NODES].partition_broadcast(P))
+        for c in range(CHUNKS):
+            o_codes = stage.tile([P, CHUNK_PASSES * OUTPUTS], U32, align_bytes=64)
+            o_scales = stage.tile([P, CHUNK_PASSES * OUTPUTS], U8, align_bytes=64)
+            stage_pair(w0[HIDDEN:NODES, :], c, o_codes, o_scales)
+            if c == 0:
+                multiply_hidden(*previous)
+                nc.vector.tensor_copy(
+                    out=h_grouped[:], in_=h_planes[:].rearrange("p t b -> p b t")
                 )
-            result = stage.tile([P, OUTPUTS], F32, bufs=2)
-            if b == 0:
-                nc.vector.tensor_copy(out=result[:], in_=back[:])
-                nc.sync.dma_start(out=out[b * P : (b + 1) * P, :], in_=result[:])
+                quantise(nc, h_grouped[:].rearrange("p b t -> p (b t)"), h_codes, h_scales)
             else:
-                nc.scalar.copy(out=result[:], in_=back[:])
-                nc.scalar.dma_start(out=out[b * P : (b + 1) * P, :], in_=result[:])
+                multiply_outputs(*previous)
+            previous = (c, o_codes, o_scales)
+        multiply_outputs(*previous)

@@ -33,8 +33,10 @@ BANK_PASSES = 2
 CHUNK_BANKS = CHUNK_PASSES // BANK_PASSES
 VECTOR_BANK = 2
 QUANT_COLS = 2048
-RAW_BUFS = 8
 PSUM_BANKS = 8
+RAW_BUFS = 8
+PAIR_BUFS = 2
+HIDDEN_BUFS = 3
 
 FLOPS = 2 * BATCH * FEATURES * NODES + 2 * BATCH * HIDDEN * OUTPUTS
 
@@ -43,14 +45,15 @@ def flip_chunk(nc, psum, identity, raw, grouped_words):
     raw_words = raw[:].bitcast(F32)
     for bank in range(CHUNK_BANKS):
         flipped = psum.tile([P, BANK_PASSES, 2, P], F32, tag="bank")
-        for g in range(BANK_PASSES):
+        for i in range(BANK_PASSES):
+            g = bank * BANK_PASSES + i
             for u in range(2):
-                first = ((bank * BANK_PASSES + g) * 2 + u) * P
+                first = (g * 2 + u) * P
                 nc.tensor.transpose(
-                    flipped[:, g, u, :], raw_words[:, first : first + P], identity[:]
+                    flipped[:, i, u, :], raw_words[:, first : first + P], identity[:]
                 )
         dest = grouped_words[:, bank * BANK_PASSES : (bank + 1) * BANK_PASSES, :, :]
-        source = flipped[:].rearrange("p g u r -> p g r u")
+        source = flipped[:].rearrange("p i u r -> p i r u")
         if bank == VECTOR_BANK:
             nc.vector.tensor_copy(out=dest, in_=source)
         else:
@@ -72,10 +75,9 @@ def quantise(nc, grouped, codes, scales):
 def tile_spn_k_kernel(tc, x, w0, w1, biases, out):
     nc = tc.nc
     with ExitStack() as ctx:
-        ctx.enter_context(tc.manual_schedule())
         consts = ctx.enter_context(tc.tile_pool(name="consts", bufs=1))
         raws = ctx.enter_context(tc.tile_pool(name="raws", bufs=RAW_BUFS))
-        stage = ctx.enter_context(tc.tile_pool(name="stage", bufs=2))
+        stage = ctx.enter_context(tc.tile_pool(name="stage", bufs=PAIR_BUFS))
         psum = ctx.enter_context(tc.psum_pool(name="psum", bufs=PSUM_BANKS))
 
         bias_rows = consts.tile([P, P], BF16)
@@ -126,20 +128,20 @@ def tile_spn_k_kernel(tc, x, w0, w1, biases, out):
         def stage_pair(rows, c, codes, scales):
             pair_grouped = stage.tile([P, PAIR * CHUNK], BF16, align_bytes=64)
             pair_words = pair_grouped[:].bitcast(F32).rearrange(
-                "p (g b r u) -> p g b r u", b=PAIR, r=P, u=2
+                "p (g s r u) -> p g s r u", s=PAIR, r=P, u=2
             )
-            for b in range(PAIR):
-                raw = load(rows[b * P : (b + 1) * P, :], c)
-                flip_chunk(nc, psum, ident_f32, raw, pair_words[:, :, b, :, :])
+            for s in range(PAIR):
+                raw = load(rows[s * P : (s + 1) * P, :], c)
+                flip_chunk(nc, psum, ident_f32, raw, pair_words[:, :, s, :, :])
             quantise(nc, pair_grouped, codes, scales)
 
         def stage_hidden(n, c):
-            w_grouped = stage.tile([P, CHUNK], BF16, align_bytes=64, bufs=3)
+            w_grouped = stage.tile([P, CHUNK], BF16, align_bytes=64, bufs=HIDDEN_BUFS)
             w_words = w_grouped[:].bitcast(F32).rearrange("p (g r u) -> p g r u", r=P, u=2)
             raw = load(w0[n * P : (n + 1) * P, :], c)
             flip_chunk(nc, psum, ident_f32, raw, w_words)
-            w_codes = stage.tile([P, CHUNK_PASSES * P], U32, align_bytes=64, bufs=3)
-            w_scales = stage.tile([P, CHUNK_PASSES * P], U8, align_bytes=64, bufs=3)
+            w_codes = stage.tile([P, CHUNK_PASSES * P], U32, align_bytes=64, bufs=HIDDEN_BUFS)
+            w_scales = stage.tile([P, CHUNK_PASSES * P], U8, align_bytes=64, bufs=HIDDEN_BUFS)
             quantise(nc, w_grouped, w_codes, w_scales)
             return w_codes, w_scales
 
@@ -203,28 +205,29 @@ def tile_spn_k_kernel(tc, x, w0, w1, biases, out):
                     )
                     nc.sync.dma_start(out=out[b * P : (b + 1) * P, :], in_=result[:])
 
-        previous = None
+        due_hidden = None
         for c in range(CHUNKS):
             cols = slice(c * CHUNK_PASSES * BATCH, (c + 1) * CHUNK_PASSES * BATCH)
             stage_pair(x, c, x_codes[:, cols], x_scales[:, cols])
             for n in range(HIDDEN_BLOCKS):
-                current = (n, c) + stage_hidden(n, c)
-                if previous is not None:
-                    multiply_hidden(*previous)
-                previous = current
+                staged = (n, c) + stage_hidden(n, c)
+                if due_hidden is not None:
+                    multiply_hidden(*due_hidden)
+                due_hidden = staged
 
         nc.sync.dma_start(out=out_bias[:], in_=biases[HIDDEN:NODES].partition_broadcast(P))
+        due_outputs = None
         for c in range(CHUNKS):
             o_codes = stage.tile([P, CHUNK_PASSES * OUTPUTS], U32, align_bytes=64)
             o_scales = stage.tile([P, CHUNK_PASSES * OUTPUTS], U8, align_bytes=64)
             stage_pair(w0[HIDDEN:NODES, :], c, o_codes, o_scales)
-            if c == 0:
-                multiply_hidden(*previous)
+            if due_outputs is None:
+                multiply_hidden(*due_hidden)
                 nc.vector.tensor_copy(
                     out=h_grouped[:], in_=h_planes[:].rearrange("p t b -> p b t")
                 )
                 quantise(nc, h_grouped[:].rearrange("p b t -> p (b t)"), h_codes, h_scales)
             else:
-                multiply_outputs(*previous)
-            previous = (c, o_codes, o_scales)
-        multiply_outputs(*previous)
+                multiply_outputs(*due_outputs)
+            due_outputs = (c, o_codes, o_scales)
+        multiply_outputs(*due_outputs)

@@ -14,6 +14,8 @@ ALU = mybir.AluOpType
 P = 128
 PACK = 4
 K_PASS = P * PACK
+WORDS = PACK // 2
+MX_ALIGN = 64
 
 BATCH = 256
 FEATURES = 16384
@@ -44,13 +46,13 @@ FLOPS = 2 * BATCH * FEATURES * NODES + 2 * BATCH * HIDDEN * OUTPUTS
 def flip_chunk(nc, psum, identity, raw, grouped_words):
     raw_words = raw[:].bitcast(F32)
     for bank in range(CHUNK_BANKS):
-        flipped = psum.tile([P, BANK_PASSES, 2, P], F32, tag="bank")
+        flipped = psum.tile([P, BANK_PASSES, WORDS, P], F32, tag="bank")
         for i in range(BANK_PASSES):
             g = bank * BANK_PASSES + i
-            for u in range(2):
-                first = (g * 2 + u) * P
+            for u in range(WORDS):
+                first_word = (g * WORDS + u) * P
                 nc.tensor.transpose(
-                    flipped[:, i, u, :], raw_words[:, first : first + P], identity[:]
+                    flipped[:, i, u, :], raw_words[:, first_word : first_word + P], identity[:]
                 )
         dest = grouped_words[:, bank * BANK_PASSES : (bank + 1) * BANK_PASSES, :, :]
         source = flipped[:].rearrange("p i u r -> p i r u")
@@ -63,18 +65,19 @@ def flip_chunk(nc, psum, identity, raw, grouped_words):
 def quantise(nc, grouped, codes, scales):
     total = grouped.shape[1]
     width = min(QUANT_COLS, total)
-    for first in range(0, total, width):
-        words = slice(first // PACK, (first + width) // PACK)
+    for first_col in range(0, total, width):
+        words = slice(first_col // PACK, (first_col + width) // PACK)
         nc.vector.quantize_mx(
             out=codes[:, words].bitcast(FP8X4),
             scales=scales[:, words],
-            in_=grouped[:, first : first + width],
+            in_=grouped[:, first_col : first_col + width],
         )
 
 
 def tile_spn_k_kernel(tc, x, w0, w1, biases, out):
     nc = tc.nc
     with ExitStack() as ctx:
+        ctx.enter_context(tc.manual_schedule())
         consts = ctx.enter_context(tc.tile_pool(name="consts", bufs=1))
         raws = ctx.enter_context(tc.tile_pool(name="raws", bufs=RAW_BUFS))
         stage = ctx.enter_context(tc.tile_pool(name="stage", bufs=PAIR_BUFS))
@@ -87,11 +90,11 @@ def tile_spn_k_kernel(tc, x, w0, w1, biases, out):
         ident_bf16 = consts.tile([P, P], BF16)
         make_identity(nc, ident_bf16[:])
 
+        w1_raw = consts.tile([P, PAIR, HIDDEN], BF16)
+        nc.sync.dma_start(out=w1_raw[:], in_=w1.rearrange("(j p) k -> p j k", p=P))
         nc.sync.dma_start(
             out=bias_rows[0:NODE_BLOCKS, :], in_=biases.rearrange("(n p) -> n p", p=P)
         )
-        w1_raw = consts.tile([P, PAIR, HIDDEN], BF16)
-        nc.sync.dma_start(out=w1_raw[:], in_=w1.rearrange("(j p) h -> p j h", p=P))
 
         bias_flipped = psum.tile([P, P], BF16, tag="bank")
         nc.tensor.transpose(bias_flipped[:], bias_rows[:], ident_bf16[:])
@@ -104,20 +107,20 @@ def tile_spn_k_kernel(tc, x, w0, w1, biases, out):
                 nc.tensor.transpose(
                     w1_flipped[:, j, t, :], w1_raw[:, j, t * P : (t + 1) * P], ident_bf16[:]
                 )
-        w1_grouped = consts.tile([P, PAIR, P, PACK], BF16, align_bytes=64)
+        w1_grouped = consts.tile([P, PAIR, P, PACK], BF16, align_bytes=MX_ALIGN)
         nc.vector.tensor_copy(
             out=w1_grouped[:], in_=w1_flipped[:].rearrange("p j t o -> p j o t")
         )
-        w1_codes = consts.tile([P, OUTPUTS], U32, align_bytes=64)
-        w1_scales = consts.tile([P, OUTPUTS], U8, align_bytes=64)
+        w1_codes = consts.tile([P, OUTPUTS], U32, align_bytes=MX_ALIGN)
+        w1_scales = consts.tile([P, OUTPUTS], U8, align_bytes=MX_ALIGN)
         quantise(nc, w1_grouped[:].rearrange("p j o t -> p (j o t)"), w1_codes, w1_scales)
 
-        x_codes = consts.tile([P, PASSES * BATCH], U32, align_bytes=64)
-        x_scales = consts.tile([P, PASSES * BATCH], U8, align_bytes=64)
+        x_codes = consts.tile([P, PASSES * BATCH], U32, align_bytes=MX_ALIGN)
+        x_scales = consts.tile([P, PASSES * BATCH], U8, align_bytes=MX_ALIGN)
         h_planes = consts.tile([P, PACK, BATCH], BF16)
-        h_grouped = consts.tile([P, BATCH, PACK], BF16, align_bytes=64)
-        h_codes = consts.tile([P, BATCH], U32, align_bytes=64)
-        h_scales = consts.tile([P, BATCH], U8, align_bytes=64)
+        h_grouped = consts.tile([P, BATCH, PACK], BF16, align_bytes=MX_ALIGN)
+        h_codes = consts.tile([P, BATCH], U32, align_bytes=MX_ALIGN)
+        h_scales = consts.tile([P, BATCH], U8, align_bytes=MX_ALIGN)
         out_bias = consts.tile([P, OUTPUTS], BF16)
 
         def load(rows, c):
@@ -126,9 +129,9 @@ def tile_spn_k_kernel(tc, x, w0, w1, biases, out):
             return raw
 
         def stage_pair(rows, c, codes, scales):
-            pair_grouped = stage.tile([P, PAIR * CHUNK], BF16, align_bytes=64)
+            pair_grouped = stage.tile([P, PAIR * CHUNK], BF16, align_bytes=MX_ALIGN)
             pair_words = pair_grouped[:].bitcast(F32).rearrange(
-                "p (g s r u) -> p g s r u", s=PAIR, r=P, u=2
+                "p (g s r u) -> p g s r u", s=PAIR, r=P, u=WORDS
             )
             for s in range(PAIR):
                 raw = load(rows[s * P : (s + 1) * P, :], c)
@@ -136,12 +139,12 @@ def tile_spn_k_kernel(tc, x, w0, w1, biases, out):
             quantise(nc, pair_grouped, codes, scales)
 
         def stage_hidden(n, c):
-            w_grouped = stage.tile([P, CHUNK], BF16, align_bytes=64, bufs=HIDDEN_BUFS)
-            w_words = w_grouped[:].bitcast(F32).rearrange("p (g r u) -> p g r u", r=P, u=2)
+            w_grouped = stage.tile([P, CHUNK], BF16, align_bytes=MX_ALIGN, bufs=HIDDEN_BUFS)
+            w_words = w_grouped[:].bitcast(F32).rearrange("p (g r u) -> p g r u", r=P, u=WORDS)
             raw = load(w0[n * P : (n + 1) * P, :], c)
             flip_chunk(nc, psum, ident_f32, raw, w_words)
-            w_codes = stage.tile([P, CHUNK_PASSES * P], U32, align_bytes=64, bufs=HIDDEN_BUFS)
-            w_scales = stage.tile([P, CHUNK_PASSES * P], U8, align_bytes=64, bufs=HIDDEN_BUFS)
+            w_codes = stage.tile([P, CHUNK_PASSES * P], U32, align_bytes=MX_ALIGN, bufs=HIDDEN_BUFS)
+            w_scales = stage.tile([P, CHUNK_PASSES * P], U8, align_bytes=MX_ALIGN, bufs=HIDDEN_BUFS)
             quantise(nc, w_grouped, w_codes, w_scales)
             return w_codes, w_scales
 
@@ -179,11 +182,11 @@ def tile_spn_k_kernel(tc, x, w0, w1, biases, out):
                     out_sum = psum.tile([P, OUTPUTS], F32, tag="bank")
                     out_sums[b] = out_sum
                 for g in range(CHUNK_PASSES):
-                    first = (c * CHUNK_PASSES + g) * BATCH + b * P
+                    first_row = (c * CHUNK_PASSES + g) * BATCH + b * P
                     nc.tensor.matmul_mx(
                         out=out_sums[b][:],
-                        lhsT=x_codes[:, first : first + P].bitcast(FP8X4),
-                        lhsT_scale=x_scales[:, first : first + P],
+                        lhsT=x_codes[:, first_row : first_row + P].bitcast(FP8X4),
+                        lhsT_scale=x_scales[:, first_row : first_row + P],
                         rhs=o_codes[:, g * OUTPUTS : (g + 1) * OUTPUTS].bitcast(FP8X4),
                         rhs_scale=o_scales[:, g * OUTPUTS : (g + 1) * OUTPUTS],
                         start=(c == 0 and g == 0),
@@ -218,15 +221,15 @@ def tile_spn_k_kernel(tc, x, w0, w1, biases, out):
         nc.sync.dma_start(out=out_bias[:], in_=biases[HIDDEN:NODES].partition_broadcast(P))
         due_outputs = None
         for c in range(CHUNKS):
-            o_codes = stage.tile([P, CHUNK_PASSES * OUTPUTS], U32, align_bytes=64)
-            o_scales = stage.tile([P, CHUNK_PASSES * OUTPUTS], U8, align_bytes=64)
+            o_codes = stage.tile([P, CHUNK_PASSES * OUTPUTS], U32, align_bytes=MX_ALIGN)
+            o_scales = stage.tile([P, CHUNK_PASSES * OUTPUTS], U8, align_bytes=MX_ALIGN)
             stage_pair(w0[HIDDEN:NODES, :], c, o_codes, o_scales)
             if due_outputs is None:
                 multiply_hidden(*due_hidden)
                 nc.vector.tensor_copy(
-                    out=h_grouped[:], in_=h_planes[:].rearrange("p t b -> p b t")
+                    out=h_grouped[:], in_=h_planes[:].rearrange("p t r -> p r t")
                 )
-                quantise(nc, h_grouped[:].rearrange("p b t -> p (b t)"), h_codes, h_scales)
+                quantise(nc, h_grouped[:].rearrange("p r t -> p (r t)"), h_codes, h_scales)
             else:
                 multiply_outputs(*due_outputs)
             due_outputs = (c, o_codes, o_scales)

@@ -101,6 +101,19 @@ def tile_spn_k_kernel(tc, x, w0, w1, biases, out):
         bias_cols = consts.tile([P, NODE_BLOCKS], F32)
         nc.vector.tensor_copy(out=bias_cols[:], in_=bias_flipped[:, 0:NODE_BLOCKS])
 
+        bias_spread = psum.tile([P, OUTPUTS], F32, tag="bank")
+        for j in range(PAIR):
+            row = HIDDEN_BLOCKS + j
+            nc.tensor.matmul(
+                bias_spread[:, j * P : (j + 1) * P],
+                lhsT=ident_bf16[:, row : row + 1].to_broadcast([P, P]),
+                rhs=bias_rows[:],
+                start=True,
+                stop=True,
+            )
+        out_bias = consts.tile([P, OUTPUTS], F32)
+        nc.vector.tensor_copy(out=out_bias[:], in_=bias_spread[:])
+
         w1_flipped = psum.tile([P, PAIR, PACK, P], BF16, tag="bank")
         for j in range(PAIR):
             for t in range(PACK):
@@ -121,7 +134,6 @@ def tile_spn_k_kernel(tc, x, w0, w1, biases, out):
         h_grouped = consts.tile([P, BATCH, PACK], BF16, align_bytes=MX_ALIGN)
         h_codes = consts.tile([P, BATCH], U32, align_bytes=MX_ALIGN)
         h_scales = consts.tile([P, BATCH], U8, align_bytes=MX_ALIGN)
-        out_bias = consts.tile([P, OUTPUTS], BF16)
 
         def load(rows, c):
             raw = raws.tile([P, CHUNK], BF16)
@@ -218,7 +230,6 @@ def tile_spn_k_kernel(tc, x, w0, w1, biases, out):
                     multiply_hidden(*due_hidden)
                 due_hidden = staged
 
-        nc.sync.dma_start(out=out_bias[:], in_=biases[HIDDEN:NODES].partition_broadcast(P))
         due_outputs = None
         for c in range(CHUNKS):
             o_codes = stage.tile([P, CHUNK_PASSES * OUTPUTS], U32, align_bytes=MX_ALIGN)

@@ -8,7 +8,6 @@ BF16 = mybir.dt.bfloat16
 U32 = mybir.dt.uint32
 U8 = mybir.dt.uint8
 FP8X4 = mybir.dt.float8_e4m3fn_x4
-ACT = mybir.ActivationFunctionType
 ALU = mybir.AluOpType
 
 P = 128
@@ -24,54 +23,27 @@ HIDDEN = 512
 OUTPUTS = NODES - HIDDEN
 
 PAIR = 2
-NODE_BLOCKS = NODES // P
-HIDDEN_BLOCKS = HIDDEN // P
+PAIR_ROWS = PAIR * P
+HIDDEN_PAIRS = HIDDEN // PAIR_ROWS
 
 PASSES = FEATURES // K_PASS
-CHUNK = 4096
-CHUNKS = FEATURES // CHUNK
-CHUNK_PASSES = CHUNK // K_PASS
-BANK_PASSES = 2
-CHUNK_BANKS = CHUNK_PASSES // BANK_PASSES
-VECTOR_BANK = 2
-QUANT_COLS = 2048
+PLAN = ((0, 4), (4, 4), (3, 0, 8), (8, 8), (3, 8, 8), (16, 8), (24, 8), (3, 16, 8), (3, 24, 4), (3, 28, 4))
+AHEAD = 2
+LAG = 8
+FINISH = 2
+QUANT_PASSES = 2
+RUN_BANKS = 8
+PRODUCTS_PER_BANK = 2
+VECTOR_EVERY = 8
+
+BANK_WORDS = PAIR_ROWS * WORDS
+
 PSUM_BANKS = 8
-RAW_BUFS = 8
-PAIR_BUFS = 2
-HIDDEN_BUFS = 3
+RAW_BUFS = 9
+GROUPED_BUFS = 2
+CODES_BUFS = 4
 
 FLOPS = 2 * BATCH * FEATURES * NODES + 2 * BATCH * HIDDEN * OUTPUTS
-
-
-def flip_chunk(nc, psum, identity, raw, grouped_words):
-    raw_words = raw[:].bitcast(F32)
-    for bank in range(CHUNK_BANKS):
-        flipped = psum.tile([P, BANK_PASSES, WORDS, P], F32, tag="bank")
-        for i in range(BANK_PASSES):
-            g = bank * BANK_PASSES + i
-            for u in range(WORDS):
-                first_word = (g * WORDS + u) * P
-                nc.tensor.transpose(
-                    flipped[:, i, u, :], raw_words[:, first_word : first_word + P], identity[:]
-                )
-        dest = grouped_words[:, bank * BANK_PASSES : (bank + 1) * BANK_PASSES, :, :]
-        source = flipped[:].rearrange("p i u r -> p i r u")
-        if bank == VECTOR_BANK:
-            nc.vector.tensor_copy(out=dest, in_=source)
-        else:
-            nc.scalar.copy(out=dest, in_=source)
-
-
-def quantise(nc, grouped, codes, scales):
-    total = grouped.shape[1]
-    width = min(QUANT_COLS, total)
-    for first_col in range(0, total, width):
-        words = slice(first_col // PACK, (first_col + width) // PACK)
-        nc.vector.quantize_mx(
-            out=codes[:, words].bitcast(FP8X4),
-            scales=scales[:, words],
-            in_=grouped[:, first_col : first_col + width],
-        )
 
 
 def tile_spn_k_kernel(tc, x, w0, w1, biases, out):
@@ -80,168 +52,261 @@ def tile_spn_k_kernel(tc, x, w0, w1, biases, out):
         ctx.enter_context(tc.manual_schedule())
         consts = ctx.enter_context(tc.tile_pool(name="consts", bufs=1))
         raws = ctx.enter_context(tc.tile_pool(name="raws", bufs=RAW_BUFS))
-        stage = ctx.enter_context(tc.tile_pool(name="stage", bufs=PAIR_BUFS))
+        groups = ctx.enter_context(tc.tile_pool(name="groups", bufs=GROUPED_BUFS))
+        codes_pool = ctx.enter_context(tc.tile_pool(name="codes", bufs=CODES_BUFS))
         psum = ctx.enter_context(tc.psum_pool(name="psum", bufs=PSUM_BANKS))
 
-        bias_rows = consts.tile([P, P], BF16)
-        nc.vector.memset(bias_rows[:], 0.0)
+        pairs = [x] + [w0[j * PAIR_ROWS : (j + 1) * PAIR_ROWS, :] for j in range(NODES // PAIR_ROWS)]
+        def load(j, first, passes):
+            tiles = []
+            cols = slice(first * K_PASS, (first + passes) * K_PASS)
+            for b in range(PAIR):
+                raw = raws.tile([P, passes * K_PASS], BF16)
+                nc.sync.dma_start(out=raw[:], in_=pairs[j][b * P : (b + 1) * P, cols])
+                tiles.append(raw)
+            return tiles
+
+        items = []
+        for spec in PLAN:
+            if len(spec) == 3:
+                items.append(spec)
+            else:
+                items.extend((j,) + spec for j in range(3))
+        hidden_last = max(m for m, it in enumerate(items) if it[0] in (1, 2))
+        loaded = [load(*item) for item in items[:AHEAD]]
+
         ident_f32 = consts.tile([P, P], F32)
         make_identity(nc, ident_f32[:])
         ident_bf16 = consts.tile([P, P], BF16)
         make_identity(nc, ident_bf16[:])
+        bias_rows = consts.tile([P, P], BF16)
+        nc.vector.memset(bias_rows[:], 0.0)
+        nc.scalar.dma_start(
+            out=bias_rows[0 : NODES // P, :], in_=biases.rearrange("(n p) -> n p", p=P)
+        )
+        bias_cols = consts.tile([P, HIDDEN // P], F32)
+        out_bias = consts.tile([P, OUTPUTS], F32)
 
         w1_raw = consts.tile([P, PAIR, HIDDEN], BF16)
-        nc.sync.dma_start(out=w1_raw[:], in_=w1.rearrange("(j p) k -> p j k", p=P))
-        nc.sync.dma_start(
-            out=bias_rows[0:NODE_BLOCKS, :], in_=biases.rearrange("(n p) -> n p", p=P)
-        )
-
-        bias_flipped = psum.tile([P, P], BF16, tag="bank")
-        nc.tensor.transpose(bias_flipped[:], bias_rows[:], ident_bf16[:])
-        bias_cols = consts.tile([P, NODE_BLOCKS], F32)
-        nc.vector.tensor_copy(out=bias_cols[:], in_=bias_flipped[:, 0:NODE_BLOCKS])
-
-        bias_spread = psum.tile([P, OUTPUTS], F32, tag="bank")
-        for j in range(PAIR):
-            row = HIDDEN_BLOCKS + j
-            nc.tensor.matmul(
-                bias_spread[:, j * P : (j + 1) * P],
-                lhsT=ident_bf16[:, row : row + 1].to_broadcast([P, P]),
-                rhs=bias_rows[:],
-                start=True,
-                stop=True,
-            )
-        out_bias = consts.tile([P, OUTPUTS], F32)
-        nc.vector.tensor_copy(out=out_bias[:], in_=bias_spread[:])
-
-        w1_flipped = psum.tile([P, PAIR, PACK, P], BF16, tag="bank")
-        for j in range(PAIR):
-            for t in range(PACK):
-                nc.tensor.transpose(
-                    w1_flipped[:, j, t, :], w1_raw[:, j, t * P : (t + 1) * P], ident_bf16[:]
-                )
         w1_grouped = consts.tile([P, PAIR, P, PACK], BF16, align_bytes=MX_ALIGN)
-        nc.vector.tensor_copy(
-            out=w1_grouped[:], in_=w1_flipped[:].rearrange("p j t o -> p j o t")
-        )
         w1_codes = consts.tile([P, OUTPUTS], U32, align_bytes=MX_ALIGN)
         w1_scales = consts.tile([P, OUTPUTS], U8, align_bytes=MX_ALIGN)
-        quantise(nc, w1_grouped[:].rearrange("p j o t -> p (j o t)"), w1_codes, w1_scales)
-
-        x_codes = consts.tile([P, PASSES * BATCH], U32, align_bytes=MX_ALIGN)
-        x_scales = consts.tile([P, PASSES * BATCH], U8, align_bytes=MX_ALIGN)
+        out_acc = consts.tile([P, PAIR, OUTPUTS], F32)
         h_planes = consts.tile([P, PACK, BATCH], BF16)
         h_grouped = consts.tile([P, BATCH, PACK], BF16, align_bytes=MX_ALIGN)
         h_codes = consts.tile([P, BATCH], U32, align_bytes=MX_ALIGN)
         h_scales = consts.tile([P, BATCH], U8, align_bytes=MX_ALIGN)
+        hidden_acc = consts.tile([P, HIDDEN // P, BATCH], F32)
 
-        def load(rows, c):
-            raw = raws.tile([P, CHUNK], BF16)
-            nc.sync.dma_start(out=raw[:], in_=rows[:, c * CHUNK : (c + 1) * CHUNK])
-            return raw
+        def spread_bias():
+            flipped = psum.tile([P, P], BF16, tag="bank")
+            nc.tensor.transpose(flipped[:], bias_rows[:], ident_bf16[:])
+            nc.vector.tensor_copy(out=bias_cols[:], in_=flipped[:, 0 : HIDDEN // P])
+            spread = psum.tile([P, OUTPUTS], F32, tag="bank")
+            for j in range(PAIR):
+                row = HIDDEN // P + j
+                nc.tensor.matmul(
+                    spread[:, j * P : (j + 1) * P],
+                    lhsT=ident_bf16[:, row : row + 1].to_broadcast([P, P]),
+                    rhs=bias_rows[:],
+                    start=True,
+                    stop=True,
+                )
+            nc.vector.tensor_copy(out=out_bias[:], in_=spread[:])
 
-        def stage_pair(rows, c, codes, scales):
-            pair_grouped = stage.tile([P, PAIR * CHUNK], BF16, align_bytes=MX_ALIGN)
-            pair_words = pair_grouped[:].bitcast(F32).rearrange(
-                "p (g s r u) -> p g s r u", s=PAIR, r=P, u=WORDS
+        def stage_w1():
+            w1_flipped = psum.tile([P, PAIR, PACK, P], BF16, tag="bank")
+            for j in range(PAIR):
+                for t in range(PACK):
+                    nc.tensor.transpose(
+                        w1_flipped[:, j, t, :], w1_raw[:, j, t * P : (t + 1) * P], ident_bf16[:]
+                    )
+            nc.scalar.copy(out=w1_grouped[:], in_=w1_flipped[:].rearrange("p j t o -> p j o t"))
+
+        def quantise_w1():
+            nc.vector.quantize_mx(
+                out=w1_codes[:].bitcast(FP8X4),
+                scales=w1_scales[:],
+                in_=w1_grouped[:].rearrange("p j o t -> p (j o t)"),
             )
-            for s in range(PAIR):
-                raw = load(rows[s * P : (s + 1) * P, :], c)
-                flip_chunk(nc, psum, ident_f32, raw, pair_words[:, :, s, :, :])
-            quantise(nc, pair_grouped, codes, scales)
 
-        def stage_hidden(n, c):
-            w_grouped = stage.tile([P, CHUNK], BF16, align_bytes=MX_ALIGN, bufs=HIDDEN_BUFS)
-            w_words = w_grouped[:].bitcast(F32).rearrange("p (g r u) -> p g r u", r=P, u=WORDS)
-            raw = load(w0[n * P : (n + 1) * P, :], c)
-            flip_chunk(nc, psum, ident_f32, raw, w_words)
-            w_codes = stage.tile([P, CHUNK_PASSES * P], U32, align_bytes=MX_ALIGN, bufs=HIDDEN_BUFS)
-            w_scales = stage.tile([P, CHUNK_PASSES * P], U8, align_bytes=MX_ALIGN, bufs=HIDDEN_BUFS)
-            quantise(nc, w_grouped, w_codes, w_scales)
-            return w_codes, w_scales
+        x_codes = consts.tile([P, PASSES, BATCH], U32, align_bytes=MX_ALIGN)
+        x_scales = consts.tile([P, PASSES, BATCH], U8, align_bytes=MX_ALIGN)
+        banks_done = []
+        due_quants = []
 
-        hidden_sums = {}
-
-        def multiply_hidden(n, c, w_codes, w_scales):
-            if c == 0:
-                hidden_sum = psum.tile([P, BATCH], F32, tag="bank")
-                hidden_sums[n] = hidden_sum
-            for g in range(CHUNK_PASSES):
-                k_pass = c * CHUNK_PASSES + g
-                nc.tensor.matmul_mx(
-                    out=hidden_sums[n][:],
-                    lhsT=w_codes[:, g * P : (g + 1) * P].bitcast(FP8X4),
-                    lhsT_scale=w_scales[:, g * P : (g + 1) * P],
-                    rhs=x_codes[:, k_pass * BATCH : (k_pass + 1) * BATCH].bitcast(FP8X4),
-                    rhs_scale=x_scales[:, k_pass * BATCH : (k_pass + 1) * BATCH],
-                    start=(k_pass == 0),
-                    stop=(k_pass == PASSES - 1),
+        def quantise_due(count):
+            for grouped, codes, scales in due_quants[:count]:
+                nc.vector.quantize_mx(
+                    out=codes.rearrange("p g r -> p (g r)").bitcast(FP8X4),
+                    scales=scales.rearrange("p g r -> p (g r)"),
+                    in_=grouped,
                 )
-            if c == CHUNKS - 1:
-                nc.scalar.activation(
-                    out=h_planes[:, n, :],
-                    in_=hidden_sums[n][:],
-                    func=ACT.Relu,
-                    bias=bias_cols[:, n : n + 1],
-                    scale=1.0,
-                )
+            due_quants[:] = due_quants[count:]
 
-        out_sums = {}
-
-        def multiply_outputs(c, o_codes, o_scales):
+        def stage(tiles, passes, codes, scales, share):
+            grouped = groups.tile([P, passes * BANK_WORDS * 2], BF16, align_bytes=MX_ALIGN)
+            words = grouped[:].bitcast(F32).rearrange(
+                "p (g b r u) -> p g b r u", g=passes, b=PAIR, u=WORDS
+            )
             for b in range(PAIR):
-                if c == 0:
-                    out_sum = psum.tile([P, OUTPUTS], F32, tag="bank")
-                    out_sums[b] = out_sum
-                for g in range(CHUNK_PASSES):
-                    first_row = (c * CHUNK_PASSES + g) * BATCH + b * P
-                    nc.tensor.matmul_mx(
-                        out=out_sums[b][:],
-                        lhsT=x_codes[:, first_row : first_row + P].bitcast(FP8X4),
-                        lhsT_scale=x_scales[:, first_row : first_row + P],
-                        rhs=o_codes[:, g * OUTPUTS : (g + 1) * OUTPUTS].bitcast(FP8X4),
-                        rhs_scale=o_scales[:, g * OUTPUTS : (g + 1) * OUTPUTS],
-                        start=(c == 0 and g == 0),
-                        stop=False,
-                    )
-                if c == CHUNKS - 1:
-                    nc.tensor.matmul_mx(
-                        out=out_sums[b][:],
-                        lhsT=h_codes[:, b * P : (b + 1) * P].bitcast(FP8X4),
-                        lhsT_scale=h_scales[:, b * P : (b + 1) * P],
-                        rhs=w1_codes[:].bitcast(FP8X4),
-                        rhs_scale=w1_scales[:],
-                        start=False,
-                        stop=True,
-                    )
-                    result = stage.tile([P, OUTPUTS], F32)
+                raw_words = tiles[b][:].bitcast(F32)
+                for g in range(0, passes, 2):
+                    flipped = psum.tile([P, 2, WORDS, P], F32, tag="bank")
+                    for i in range(2):
+                        for u in range(WORDS):
+                            first_word = ((g + i) * WORDS + u) * P
+                            nc.tensor.transpose(
+                                flipped[:, i, u, :],
+                                raw_words[:, first_word : first_word + P],
+                                ident_f32[:],
+                            )
+                    source = flipped[:].rearrange("p i u r -> p i r u")
+                    dest = words[:, g : g + 2, b]
+                    if len(banks_done) % VECTOR_EVERY == 2 or (share and b == 1 and g % 4 == 2):
+                        nc.vector.tensor_copy(out=dest, in_=source)
+                    else:
+                        nc.scalar.copy(out=dest, in_=source)
+                    banks_done.append(g)
+                    if len(banks_done) % 2 == 0:
+                        quantise_due(1)
+            for g in range(0, passes, QUANT_PASSES):
+                due_quants.append((
+                    grouped[:, g * BANK_WORDS * 2 : (g + QUANT_PASSES) * BANK_WORDS * 2],
+                    codes[:, g : g + QUANT_PASSES, :],
+                    scales[:, g : g + QUANT_PASSES, :],
+                ))
+
+        due_products = []
+        due_adds = []
+
+        def product(item, codes, scales, sums, block, g):
+            j, first, passes = item
+            k_pass = first + g
+            rows = slice(block * P, (block + 1) * P)
+            x_side = (x_codes[:, k_pass, :], x_scales[:, k_pass, :])
+            w_side = (codes[:, g, :], scales[:, g, :])
+            still, moving = (x_side, w_side) if j == 3 else (w_side, x_side)
+            last = g == passes - 1
+            final = first + passes == PASSES
+            if j == 3 and final and g == 0:
+                multiply_h(sums, block)
+            nc.tensor.matmul_mx(
+                out=sums,
+                lhsT=still[0][:, rows].bitcast(FP8X4),
+                lhsT_scale=still[1][:, rows],
+                rhs=moving[0].bitcast(FP8X4),
+                rhs_scale=moving[1],
+                start=(g == 0 and not (j == 3 and final)),
+                stop=last,
+            )
+            if last and block == PAIR - 1:
+                due_adds.append((j, open_sums[item], first == 0, final))
+
+        open_sums = {}
+
+        def multiply(lag, limit):
+            count = 0
+            for item, codes, scales, block, g, staged in due_products:
+                if count == limit or len(banks_done) - staged < lag:
+                    break
+                count += 1
+                if item not in open_sums:
+                    some_sum = psum.tile([P, PAIR, BATCH], F32, tag="bank")
+                    open_sums[item] = some_sum
+                product(item, codes, scales, open_sums[item][:, block, :], block, g)
+            due_products[:] = due_products[count:]
+
+        def add_due():
+            for j, sums, is_first, is_last in due_adds:
+                if j == 3:
+                    for b in range(PAIR):
+                        other = out_bias[:] if is_first else out_acc[:, b, :]
+                        if is_last:
+                            result = groups.tile([P, OUTPUTS], F32, bufs=2)
+                            dest = result[:]
+                        else:
+                            dest = out_acc[:, b, :]
+                        nc.vector.tensor_tensor(
+                            out=dest, in0=sums[:, b, :], in1=other, op=ALU.add
+                        )
+                        if is_last:
+                            queue = nc.sync if b == 0 else nc.scalar
+                            queue.dma_start(out=out[b * P : (b + 1) * P, :], in_=dest)
+                    continue
+                blocks = slice((j - 1) * PAIR, j * PAIR)
+                if is_first:
+                    for b in range(PAIR):
+                        n = (j - 1) * PAIR + b
+                        nc.vector.tensor_scalar(
+                            out=hidden_acc[:, n, :],
+                            in0=sums[:, b, :],
+                            scalar1=bias_cols[:, n : n + 1],
+                            scalar2=None,
+                            op0=ALU.add,
+                        )
+                else:
                     nc.vector.tensor_tensor(
-                        out=result[:], in0=out_sums[b][:], in1=out_bias[:], op=ALU.add
+                        out=hidden_acc[:, blocks, :],
+                        in0=sums[:],
+                        in1=hidden_acc[:, blocks, :],
+                        op=ALU.add,
                     )
-                    nc.sync.dma_start(out=out[b * P : (b + 1) * P, :], in_=result[:])
+                if is_last:
+                    nc.vector.tensor_scalar_max(
+                        h_planes[:, blocks, :], hidden_acc[:, blocks, :], 0.0
+                    )
+            due_adds.clear()
 
-        due_hidden = None
-        for c in range(CHUNKS):
-            cols = slice(c * CHUNK_PASSES * BATCH, (c + 1) * CHUNK_PASSES * BATCH)
-            stage_pair(x, c, x_codes[:, cols], x_scales[:, cols])
-            for n in range(HIDDEN_BLOCKS):
-                staged = (n, c) + stage_hidden(n, c)
-                if due_hidden is not None:
-                    multiply_hidden(*due_hidden)
-                due_hidden = staged
+        def multiply_h(sums, b):
+            nc.tensor.matmul_mx(
+                out=sums,
+                lhsT=h_codes[:, b * P : (b + 1) * P].bitcast(FP8X4),
+                lhsT_scale=h_scales[:, b * P : (b + 1) * P],
+                rhs=w1_codes[:].bitcast(FP8X4),
+                rhs_scale=w1_scales[:],
+                start=True,
+                stop=False,
+            )
 
-        due_outputs = None
-        for c in range(CHUNKS):
-            o_codes = stage.tile([P, CHUNK_PASSES * OUTPUTS], U32, align_bytes=MX_ALIGN)
-            o_scales = stage.tile([P, CHUNK_PASSES * OUTPUTS], U8, align_bytes=MX_ALIGN)
-            stage_pair(w0[HIDDEN:NODES, :], c, o_codes, o_scales)
-            if due_outputs is None:
-                multiply_hidden(*due_hidden)
-                nc.vector.tensor_copy(
-                    out=h_grouped[:], in_=h_planes[:].rearrange("p t r -> p r t")
-                )
-                quantise(nc, h_grouped[:].rearrange("p r t -> p (r t)"), h_codes, h_scales)
+        def finish_h():
+            nc.vector.tensor_copy(out=h_grouped[:], in_=h_planes[:].rearrange("p t r -> p r t"))
+            nc.vector.quantize_mx(
+                out=h_codes[:].bitcast(FP8X4),
+                scales=h_scales[:],
+                in_=h_grouped[:].rearrange("p r t -> p (r t)"),
+            )
+
+        for m, item in enumerate(items):
+            j, first, passes = item
+            while len(loaded) < min(m + 1 + AHEAD, len(items)):
+                loaded.append(load(*items[len(loaded)]))
+            last_item = m == len(items) - 1
+            if j == 0:
+                codes = x_codes[:, first : first + passes, :]
+                scales = x_scales[:, first : first + passes, :]
             else:
-                multiply_outputs(*due_outputs)
-            due_outputs = (c, o_codes, o_scales)
-        multiply_outputs(*due_outputs)
+                codes_tile = codes_pool.tile([P, passes, PAIR_ROWS], U32, align_bytes=MX_ALIGN)
+                scales_tile = codes_pool.tile([P, passes, PAIR_ROWS], U8, align_bytes=MX_ALIGN)
+                codes, scales = codes_tile[:], scales_tile[:]
+            stage(loaded[m], passes, codes, scales, last_item)
+            add_due()
+            if m == 2:
+                spread_bias()
+            if m == 9:
+                nc.sync.dma_start(out=w1_raw[:], in_=w1.rearrange("(j p) k -> p j k", p=P))
+            if m == 12:
+                stage_w1()
+            quantise_due(len(due_quants))
+            if m == 12:
+                quantise_w1()
+            multiply(LAG, int(PRODUCTS_PER_BANK * passes))
+            if m == hidden_last + FINISH:
+                add_due()
+                finish_h()
+            if j > 0:
+                for block in range(PAIR):
+                    for g in range(passes):
+                        due_products.append((item, codes, scales, block, g, len(banks_done)))
+        multiply(0, len(due_products))
+        add_due()

@@ -24,24 +24,33 @@ OUTPUTS = NODES - HIDDEN
 
 PAIR = 2
 PAIR_ROWS = PAIR * P
-HIDDEN_PAIRS = HIDDEN // PAIR_ROWS
+HIDDEN_BLOCKS = HIDDEN // P
+X, OUTPUT = HIDDEN_BLOCKS, HIDDEN_BLOCKS + 1
 
 PASSES = FEATURES // K_PASS
-PLAN = ((0, 4), (4, 4), (3, 0, 8), (8, 8), (3, 8, 8), (16, 8), (24, 8), (3, 16, 8), (3, 24, 4), (3, 28, 4))
-AHEAD = 2
-LAG = 8
-FINISH = 2
-QUANT_PASSES = 2
-RUN_BANKS = 8
-PRODUCTS_PER_BANK = 2
-VECTOR_EVERY = 8
-
+BANK_PASSES = 2
+BANK_COLS = P * PACK
 BANK_WORDS = PAIR_ROWS * WORDS
 
+PLAN = ((0, 8), (3, 0, 8), (8, 8), (3, 8, 8), (16, 8), (24, 8), (3, 16, 8), (3, 24, 4), (3, 28, 4))
+LOOK = 7
+TWO = 0
+HEAD = 0
+LATE = 14
+SMALL = 6
+RUN_BANKS = 8
+LAG = 8
+EDGE_LAG = 4
+VECTOR_EVERY = 6
+QLAG = 1
+TAIL = 1
+HEAD_RUN = 4
+FINISH = 2
+
 PSUM_BANKS = 8
-RAW_BUFS = 9
-GROUPED_BUFS = 2
-CODES_BUFS = 4
+RAW_BUFS = 8
+GROUPED_BUFS = (0, 3, 2)
+CODES_BUFS = (0, 5, 3)
 
 FLOPS = 2 * BATCH * FEATURES * NODES + 2 * BATCH * HIDDEN * OUTPUTS
 
@@ -52,261 +61,289 @@ def tile_spn_k_kernel(tc, x, w0, w1, biases, out):
         ctx.enter_context(tc.manual_schedule())
         consts = ctx.enter_context(tc.tile_pool(name="consts", bufs=1))
         raws = ctx.enter_context(tc.tile_pool(name="raws", bufs=RAW_BUFS))
-        groups = ctx.enter_context(tc.tile_pool(name="groups", bufs=GROUPED_BUFS))
-        codes_pool = ctx.enter_context(tc.tile_pool(name="codes", bufs=CODES_BUFS))
+        groups = ctx.enter_context(tc.tile_pool(name="groups", bufs=1))
+        coded = ctx.enter_context(tc.tile_pool(name="coded", bufs=1))
         psum = ctx.enter_context(tc.psum_pool(name="psum", bufs=PSUM_BANKS))
 
-        pairs = [x] + [w0[j * PAIR_ROWS : (j + 1) * PAIR_ROWS, :] for j in range(NODES // PAIR_ROWS)]
-        def load(j, first, passes):
-            tiles = []
-            cols = slice(first * K_PASS, (first + passes) * K_PASS)
-            for b in range(PAIR):
-                raw = raws.tile([P, passes * K_PASS], BF16)
-                nc.sync.dma_start(out=raw[:], in_=pairs[j][b * P : (b + 1) * P, cols])
-                tiles.append(raw)
-            return tiles
-
+        rows_of = [w0[n * P : (n + 1) * P, :] for n in range(HIDDEN_BLOCKS)]
+        rows_of += [x, w0[HIDDEN:NODES, :]]
         items = []
         for spec in PLAN:
             if len(spec) == 3:
-                items.append(spec)
+                items.append((OUTPUT,) + spec[1:])
             else:
-                items.extend((j,) + spec for j in range(3))
-        hidden_last = max(m for m, it in enumerate(items) if it[0] in (1, 2))
-        loaded = [load(*item) for item in items[:AHEAD]]
+                items.extend((j,) + spec for j in (X, 0, 1, 2, 3))
+        hidden_end = max(m for m, item in enumerate(items) if item[0] < HIDDEN_BLOCKS)
 
+        blocks = [
+            (m, b) for m, item in enumerate(items) for b in range(rows_of[item[0]].shape[0] // P)
+        ]
+        raw_tiles = {}
+        taken = []
+
+        def load_until(count):
+            for m, b in blocks[len(taken) : count]:
+                j, first, passes = items[m]
+                raw = raws.tile([P, passes * K_PASS], BF16, align_bytes=MX_ALIGN)
+                cols = slice(first * K_PASS, (first + passes) * K_PASS)
+                rows = rows_of[j][b * P : (b + 1) * P, cols]
+                half = passes * K_PASS // 2
+                if TWO:
+                    nc.sync.dma_start(out=raw[:, 0:half], in_=rows[:, 0:half])
+                    nc.scalar.dma_start(out=raw[:, half : 2 * half], in_=rows[:, half : 2 * half])
+                else:
+                    nc.sync.dma_start(out=raw[:], in_=rows)
+                raw_tiles[(m, b)] = raw
+                taken.append((m, b))
+
+        load_until(LOOK)
+
+        bias_rows = consts.tile([P, P], BF16)
+        nc.vector.memset(bias_rows[:], 0.0)
         ident_f32 = consts.tile([P, P], F32)
         make_identity(nc, ident_f32[:])
         ident_bf16 = consts.tile([P, P], BF16)
         make_identity(nc, ident_bf16[:])
-        bias_rows = consts.tile([P, P], BF16)
-        nc.vector.memset(bias_rows[:], 0.0)
-        nc.scalar.dma_start(
-            out=bias_rows[0 : NODES // P, :], in_=biases.rearrange("(n p) -> n p", p=P)
-        )
-        bias_cols = consts.tile([P, HIDDEN // P], F32)
+        bias_cols = consts.tile([P, HIDDEN_BLOCKS], F32)
         out_bias = consts.tile([P, OUTPUTS], F32)
 
         w1_raw = consts.tile([P, PAIR, HIDDEN], BF16)
         w1_grouped = consts.tile([P, PAIR, P, PACK], BF16, align_bytes=MX_ALIGN)
         w1_codes = consts.tile([P, OUTPUTS], U32, align_bytes=MX_ALIGN)
         w1_scales = consts.tile([P, OUTPUTS], U8, align_bytes=MX_ALIGN)
+        x_codes = consts.tile([P, PASSES, BATCH], U32, align_bytes=MX_ALIGN)
+        x_scales = consts.tile([P, PASSES, BATCH], U8, align_bytes=MX_ALIGN)
+        hidden_acc = consts.tile([P, HIDDEN_BLOCKS, BATCH], F32)
         out_acc = consts.tile([P, PAIR, OUTPUTS], F32)
         h_planes = consts.tile([P, PACK, BATCH], BF16)
         h_grouped = consts.tile([P, BATCH, PACK], BF16, align_bytes=MX_ALIGN)
         h_codes = consts.tile([P, BATCH], U32, align_bytes=MX_ALIGN)
         h_scales = consts.tile([P, BATCH], U8, align_bytes=MX_ALIGN)
-        hidden_acc = consts.tile([P, HIDDEN // P, BATCH], F32)
+
+        def load_small():
+            nc.sync.dma_start(out=w1_raw[:], in_=w1.rearrange("(j p) k -> p j k", p=P))
+            nc.sync.dma_start(
+                out=bias_rows[0 : NODES // P, :], in_=biases.rearrange("(n p) -> n p", p=P)
+            )
 
         def spread_bias():
             flipped = psum.tile([P, P], BF16, tag="bank")
             nc.tensor.transpose(flipped[:], bias_rows[:], ident_bf16[:])
-            nc.vector.tensor_copy(out=bias_cols[:], in_=flipped[:, 0 : HIDDEN // P])
-            spread = psum.tile([P, OUTPUTS], F32, tag="bank")
-            for j in range(PAIR):
-                row = HIDDEN // P + j
+            nc.vector.tensor_copy(out=bias_cols[:], in_=flipped[:, 0:HIDDEN_BLOCKS])
+            chosen = psum.tile([P, OUTPUTS], F32, tag="bank")
+            for b in range(PAIR):
+                row = HIDDEN_BLOCKS + b
                 nc.tensor.matmul(
-                    spread[:, j * P : (j + 1) * P],
+                    chosen[:, b * P : (b + 1) * P],
                     lhsT=ident_bf16[:, row : row + 1].to_broadcast([P, P]),
                     rhs=bias_rows[:],
                     start=True,
                     stop=True,
                 )
-            nc.vector.tensor_copy(out=out_bias[:], in_=spread[:])
+            nc.vector.tensor_copy(out=out_bias[:], in_=chosen[:])
+            for b in range(PAIR):
+                nc.vector.tensor_tensor(
+                    out=out_acc[:, b, :], in0=out_acc[:, b, :], in1=out_bias[:], op=ALU.add
+                )
 
-        def stage_w1():
-            w1_flipped = psum.tile([P, PAIR, PACK, P], BF16, tag="bank")
-            for j in range(PAIR):
+        def quantise(grouped, codes, scales):
+            nc.vector.quantize_mx(out=codes.bitcast(FP8X4), scales=scales, in_=grouped)
+
+        def flip_w1():
+            flipped = psum.tile([P, PAIR, PACK, P], BF16, tag="bank")
+            for b in range(PAIR):
                 for t in range(PACK):
                     nc.tensor.transpose(
-                        w1_flipped[:, j, t, :], w1_raw[:, j, t * P : (t + 1) * P], ident_bf16[:]
+                        flipped[:, b, t, :], w1_raw[:, b, t * P : (t + 1) * P], ident_bf16[:]
                     )
-            nc.scalar.copy(out=w1_grouped[:], in_=w1_flipped[:].rearrange("p j t o -> p j o t"))
+            nc.scalar.copy(out=w1_grouped[:], in_=flipped[:].rearrange("p b t o -> p b o t"))
 
-        def quantise_w1():
-            nc.vector.quantize_mx(
-                out=w1_codes[:].bitcast(FP8X4),
-                scales=w1_scales[:],
-                in_=w1_grouped[:].rearrange("p j o t -> p (j o t)"),
-            )
-
-        x_codes = consts.tile([P, PASSES, BATCH], U32, align_bytes=MX_ALIGN)
-        x_scales = consts.tile([P, PASSES, BATCH], U8, align_bytes=MX_ALIGN)
         banks_done = []
         due_quants = []
 
-        def quantise_due(count):
-            for grouped, codes, scales in due_quants[:count]:
-                nc.vector.quantize_mx(
-                    out=codes.rearrange("p g r -> p (g r)").bitcast(FP8X4),
-                    scales=scales.rearrange("p g r -> p (g r)"),
-                    in_=grouped,
-                )
+        def quantise_due(left):
+            count = max(len(due_quants) - left, 0)
+            for args in due_quants[:count]:
+                quantise(*args)
             due_quants[:] = due_quants[count:]
 
-        def stage(tiles, passes, codes, scales, share):
-            grouped = groups.tile([P, passes * BANK_WORDS * 2], BF16, align_bytes=MX_ALIGN)
+        def flat(ap):
+            return ap.rearrange("p g r -> p (g r)")
+
+        def flip(raw, b, blocks, grouped, codes, scales):
+            passes = codes.shape[1]
+            raw_words = raw[:].bitcast(F32)
             words = grouped[:].bitcast(F32).rearrange(
-                "p (g b r u) -> p g b r u", g=passes, b=PAIR, u=WORDS
+                "p (g b r u) -> p g b r u", g=passes, b=blocks, u=WORDS
             )
-            for b in range(PAIR):
-                raw_words = tiles[b][:].bitcast(F32)
-                for g in range(0, passes, 2):
-                    flipped = psum.tile([P, 2, WORDS, P], F32, tag="bank")
-                    for i in range(2):
-                        for u in range(WORDS):
-                            first_word = ((g + i) * WORDS + u) * P
-                            nc.tensor.transpose(
-                                flipped[:, i, u, :],
-                                raw_words[:, first_word : first_word + P],
-                                ident_f32[:],
-                            )
-                    source = flipped[:].rearrange("p i u r -> p i r u")
-                    dest = words[:, g : g + 2, b]
-                    if len(banks_done) % VECTOR_EVERY == 2 or (share and b == 1 and g % 4 == 2):
-                        nc.vector.tensor_copy(out=dest, in_=source)
-                    else:
-                        nc.scalar.copy(out=dest, in_=source)
-                    banks_done.append(g)
-                    if len(banks_done) % 2 == 0:
-                        quantise_due(1)
-            for g in range(0, passes, QUANT_PASSES):
-                due_quants.append((
-                    grouped[:, g * BANK_WORDS * 2 : (g + QUANT_PASSES) * BANK_WORDS * 2],
-                    codes[:, g : g + QUANT_PASSES, :],
-                    scales[:, g : g + QUANT_PASSES, :],
-                ))
+            for g in range(0, passes, BANK_PASSES):
+                span = slice(g, g + BANK_PASSES)
+                flipped = psum.tile([P, BANK_PASSES, WORDS, P], F32, tag="bank")
+                for i in range(BANK_PASSES):
+                    for u in range(WORDS):
+                        word = ((g + i) * WORDS + u) * P
+                        nc.tensor.transpose(
+                            flipped[:, i, u, :], raw_words[:, word : word + P], ident_f32[:]
+                        )
+                source = flipped[:].rearrange("p i u r -> p i r u")
+                if len(banks_done) % VECTOR_EVERY == 2:
+                    nc.vector.tensor_copy(out=words[:, span, b], in_=source)
+                else:
+                    nc.scalar.copy(out=words[:, span, b], in_=source)
+                banks_done.append(g)
+                quant_passes = 2 * PAIR // blocks
+                if b == blocks - 1 and (g + BANK_PASSES) % quant_passes == 0:
+                    start = g + BANK_PASSES - quant_passes
+                    span = slice(start, start + quant_passes)
+                    cols = slice(start * BANK_COLS * blocks, (start + quant_passes) * BANK_COLS * blocks)
+                    due_quants.append((
+                        grouped[:, cols], flat(codes[:, span, :]), flat(scales[:, span, :])
+                    ))
+                quantise_due(QLAG)
 
         due_products = []
         due_adds = []
+        open_sums = {}
 
-        def product(item, codes, scales, sums, block, g):
+        def sums_key(item):
+            return (item[0] // PAIR, item[1])
+
+        def product(item, codes, scales, b, g):
             j, first, passes = item
-            k_pass = first + g
-            rows = slice(block * P, (block + 1) * P)
-            x_side = (x_codes[:, k_pass, :], x_scales[:, k_pass, :])
+            sums = open_sums[sums_key(item)][:, b if j == OUTPUT else j % PAIR, :]
+            rows = slice(b * P, (b + 1) * P)
+            x_side = (x_codes[:, first + g, :], x_scales[:, first + g, :])
             w_side = (codes[:, g, :], scales[:, g, :])
-            still, moving = (x_side, w_side) if j == 3 else (w_side, x_side)
+            still, moving = (x_side, w_side) if j == OUTPUT else (w_side, x_side)
             last = g == passes - 1
-            final = first + passes == PASSES
-            if j == 3 and final and g == 0:
-                multiply_h(sums, block)
+            with_h = j == OUTPUT and first + passes == PASSES
             nc.tensor.matmul_mx(
                 out=sums,
                 lhsT=still[0][:, rows].bitcast(FP8X4),
                 lhsT_scale=still[1][:, rows],
                 rhs=moving[0].bitcast(FP8X4),
                 rhs_scale=moving[1],
-                start=(g == 0 and not (j == 3 and final)),
-                stop=last,
+                start=(g == 0),
+                stop=(last and not with_h),
             )
-            if last and block == PAIR - 1:
-                due_adds.append((j, open_sums[item], first == 0, final))
+            if last and with_h:
+                nc.tensor.matmul_mx(
+                    out=sums,
+                    lhsT=h_codes[:, rows].bitcast(FP8X4),
+                    lhsT_scale=h_scales[:, rows],
+                    rhs=w1_codes[:].bitcast(FP8X4),
+                    rhs_scale=w1_scales[:],
+                    start=False,
+                    stop=True,
+                )
+            if last and (b == PAIR - 1 or j in (1, 3)):
+                due_adds.append(item)
 
-        open_sums = {}
+        def multiply(lag):
+            ready = [args for args in due_products if len(banks_done) - args[-1] >= lag]
+            for item, codes, scales, b, g, staged in ready:
+                if sums_key(item) not in open_sums:
+                    sums = psum.tile([P, PAIR, PAIR_ROWS], F32, tag="bank")
+                    open_sums[sums_key(item)] = sums
+                product(item, codes, scales, b, g)
+            due_products[:] = due_products[len(ready):]
 
-        def multiply(lag, limit):
-            count = 0
-            for item, codes, scales, block, g, staged in due_products:
-                if count == limit or len(banks_done) - staged < lag:
-                    break
-                count += 1
-                if item not in open_sums:
-                    some_sum = psum.tile([P, PAIR, BATCH], F32, tag="bank")
-                    open_sums[item] = some_sum
-                product(item, codes, scales, open_sums[item][:, block, :], block, g)
-            due_products[:] = due_products[count:]
+        due_relus = []
+
+        def relu_due():
+            for n in due_relus:
+                for block in range(n, n + PAIR):
+                    nc.vector.tensor_scalar(
+                        out=h_planes[:, block, :],
+                        in0=hidden_acc[:, block, :],
+                        scalar1=bias_cols[:, block : block + 1],
+                        scalar2=0.0,
+                        op0=ALU.add,
+                        op1=ALU.max,
+                    )
+            due_relus.clear()
 
         def add_due():
-            for j, sums, is_first, is_last in due_adds:
-                if j == 3:
+            for item in due_adds:
+                j, first, passes = item
+                sums = open_sums[sums_key(item)]
+                begins, ends = first == 0, first + passes == PASSES
+                if j == OUTPUT:
                     for b in range(PAIR):
-                        other = out_bias[:] if is_first else out_acc[:, b, :]
-                        if is_last:
-                            result = groups.tile([P, OUTPUTS], F32, bufs=2)
+                        dest = out_acc[:, b, :]
+                        if ends:
+                            result = consts.tile([P, OUTPUTS], F32, name="result%d" % b)
                             dest = result[:]
+                        if begins:
+                            nc.scalar.copy(out=dest, in_=sums[:, b, :])
                         else:
-                            dest = out_acc[:, b, :]
-                        nc.vector.tensor_tensor(
-                            out=dest, in0=sums[:, b, :], in1=other, op=ALU.add
-                        )
-                        if is_last:
+                            nc.vector.tensor_tensor(
+                                out=dest, in0=sums[:, b, :], in1=out_acc[:, b, :], op=ALU.add
+                            )
+                        if ends:
                             queue = nc.sync if b == 0 else nc.scalar
                             queue.dma_start(out=out[b * P : (b + 1) * P, :], in_=dest)
-                    continue
-                blocks = slice((j - 1) * PAIR, j * PAIR)
-                if is_first:
-                    for b in range(PAIR):
-                        n = (j - 1) * PAIR + b
-                        nc.vector.tensor_scalar(
-                            out=hidden_acc[:, n, :],
-                            in0=sums[:, b, :],
-                            scalar1=bias_cols[:, n : n + 1],
-                            scalar2=None,
-                            op0=ALU.add,
-                        )
                 else:
-                    nc.vector.tensor_tensor(
-                        out=hidden_acc[:, blocks, :],
-                        in0=sums[:],
-                        in1=hidden_acc[:, blocks, :],
-                        op=ALU.add,
-                    )
-                if is_last:
-                    nc.vector.tensor_scalar_max(
-                        h_planes[:, blocks, :], hidden_acc[:, blocks, :], 0.0
-                    )
+                    n = j - 1
+                    acc = hidden_acc[:, n : n + PAIR, :]
+                    if begins:
+                        nc.scalar.copy(out=acc, in_=sums[:])
+                    else:
+                        nc.vector.tensor_tensor(out=acc, in0=sums[:], in1=acc, op=ALU.add)
+                    if ends:
+                        due_relus.append(n)
             due_adds.clear()
-
-        def multiply_h(sums, b):
-            nc.tensor.matmul_mx(
-                out=sums,
-                lhsT=h_codes[:, b * P : (b + 1) * P].bitcast(FP8X4),
-                lhsT_scale=h_scales[:, b * P : (b + 1) * P],
-                rhs=w1_codes[:].bitcast(FP8X4),
-                rhs_scale=w1_scales[:],
-                start=True,
-                stop=False,
-            )
 
         def finish_h():
             nc.vector.tensor_copy(out=h_grouped[:], in_=h_planes[:].rearrange("p t r -> p r t"))
-            nc.vector.quantize_mx(
-                out=h_codes[:].bitcast(FP8X4),
-                scales=h_scales[:],
-                in_=h_grouped[:].rearrange("p r t -> p (r t)"),
-            )
+            quantise(h_grouped[:].rearrange("p r t -> p (r t)"), h_codes[:], h_scales[:])
 
+        flushed = 0
+        done = []
         for m, item in enumerate(items):
             j, first, passes = item
-            while len(loaded) < min(m + 1 + AHEAD, len(items)):
-                loaded.append(load(*items[len(loaded)]))
-            last_item = m == len(items) - 1
-            if j == 0:
+            count = rows_of[j].shape[0] // P
+            if m == SMALL:
+                load_small()
+            if j == X:
                 codes = x_codes[:, first : first + passes, :]
                 scales = x_scales[:, first : first + passes, :]
             else:
-                codes_tile = codes_pool.tile([P, passes, PAIR_ROWS], U32, align_bytes=MX_ALIGN)
-                scales_tile = codes_pool.tile([P, passes, PAIR_ROWS], U8, align_bytes=MX_ALIGN)
+                width = count * P
+                bufs = CODES_BUFS[count]
+                codes_tile = coded.tile([P, passes, width], U32, align_bytes=MX_ALIGN, tag="codes%d" % width, bufs=bufs)
+                scales_tile = coded.tile([P, passes, width], U8, align_bytes=MX_ALIGN, tag="scales%d" % width, bufs=bufs)
                 codes, scales = codes_tile[:], scales_tile[:]
-            stage(loaded[m], passes, codes, scales, last_item)
-            add_due()
-            if m == 2:
+            grouped = groups.tile(
+                [P, passes * BANK_COLS * count], BF16, align_bytes=MX_ALIGN,
+                tag="words%d" % count, bufs=GROUPED_BUFS[count],
+            )
+            for b in range(count):
+                flip(raw_tiles[(m, b)], b, count, grouped, codes, scales)
+                done.append(b)
+                load_until(len(done) + LOOK)
+                if b == 0:
+                    add_due()
+                    relu_due()
+            if m == LATE:
                 spread_bias()
-            if m == 9:
-                nc.sync.dma_start(out=w1_raw[:], in_=w1.rearrange("(j p) k -> p j k", p=P))
-            if m == 12:
-                stage_w1()
-            quantise_due(len(due_quants))
-            if m == 12:
-                quantise_w1()
-            multiply(LAG, int(PRODUCTS_PER_BANK * passes))
-            if m == hidden_last + FINISH:
+            if m == LATE:
+                flip_w1()
+            if m == LATE:
+                quantise(w1_grouped[:].rearrange("p b o t -> p (b o t)"), w1_codes[:], w1_scales[:])
+            run = HEAD_RUN if m < HEAD else RUN_BANKS
+            edge = m >= len(items) - TAIL
+            if len(banks_done) - flushed >= run or edge:
+                multiply(EDGE_LAG if edge else LAG)
+                flushed = len(banks_done)
+            if m == hidden_end + FINISH:
                 add_due()
+                relu_due()
                 finish_h()
-            if j > 0:
-                for block in range(PAIR):
+            if j != X:
+                for b in range(PAIR if j == OUTPUT else 1):
                     for g in range(passes):
-                        due_products.append((item, codes, scales, block, g, len(banks_done)))
-        multiply(0, len(due_products))
+                        due_products.append((item, codes, scales, b, g, len(banks_done)))
+        quantise_due(0)
+        multiply(0)
         add_due()

@@ -34,6 +34,10 @@ BANK_WORDS = PAIR_ROWS * WORDS
 
 PLAN = ((0, 8), (3, 0, 8), (8, 8), (3, 8, 8), (16, 8), (24, 8), (3, 16, 8), (3, 24, 4), (3, 28, 4))
 LOOK = 7
+IDLE_COLS = 512
+FIRST_IDLE = 5
+IDLE_BLOCKS = 5
+BLOCK_IDLE = 3
 TWO = 0
 HEAD = 0
 LATE = 14
@@ -100,6 +104,17 @@ def tile_spn_k_kernel(tc, x, w0, w1, biases, out):
 
         bias_rows = consts.tile([P, P], BF16)
         nc.vector.memset(bias_rows[:], 0.0)
+        idle_rows = consts.tile([P, IDLE_COLS], BF16)
+        nc.vector.memset(idle_rows[:], 0.0)
+
+        def keep_busy(count):
+            unread = psum.tile([P, IDLE_COLS], F32, tag="bank")
+            for unused in range(count):
+                nc.tensor.matmul(
+                    unread[:], lhsT=idle_rows[:, 0:P], rhs=idle_rows[:], start=True, stop=True
+                )
+
+        keep_busy(FIRST_IDLE)
         ident_f32 = consts.tile([P, P], F32)
         make_identity(nc, ident_f32[:])
         ident_bf16 = consts.tile([P, P], BF16)
@@ -321,6 +336,8 @@ def tile_spn_k_kernel(tc, x, w0, w1, biases, out):
             for b in range(count):
                 flip(raw_tiles[(m, b)], b, count, grouped, codes, scales)
                 done.append(b)
+                if len(done) <= IDLE_BLOCKS:
+                    keep_busy(BLOCK_IDLE)
                 load_until(len(done) + LOOK)
                 if b == 0:
                     add_due()

@@ -14,7 +14,7 @@ P = 128
 PACK = 4
 K_PASS = P * PACK
 WORDS = PACK // 2
-MX_ALIGN = 64
+MX_ALIGN = 256
 
 BATCH = 256
 FEATURES = 16384

@@ -23,40 +23,51 @@ HIDDEN = 512
 OUTPUTS = NODES - HIDDEN
 
 PAIR = 2
-PAIR_ROWS = PAIR * P
 HIDDEN_BLOCKS = HIDDEN // P
-X, OUTPUT = HIDDEN_BLOCKS, HIDDEN_BLOCKS + 1
-
 PASSES = FEATURES // K_PASS
+
+X = HIDDEN_BLOCKS
+OUTPUT = HIDDEN_BLOCKS + 1
+
+ORDER = (
+    (False, 0, 8),
+    (True, 0, 8),
+    (False, 8, 8),
+    (True, 8, 8),
+    (False, 16, 8),
+    (False, 24, 8),
+    (True, 16, 8),
+    (True, 24, 4),
+    (True, 28, 4),
+)
+
 BANK_PASSES = 2
-BANK_COLS = P * PACK
-BANK_WORDS = PAIR_ROWS * WORDS
+BLOCK_COLS = P * PACK
+QUANT_COLS = 2048
 
-PLAN = ((0, 8), (3, 0, 8), (8, 8), (3, 8, 8), (16, 8), (24, 8), (3, 16, 8), (3, 24, 4), (3, 28, 4))
-LOOK = 7
-IDLE_COLS = 512
-FIRST_IDLE = 5
-IDLE_BLOCKS = 5
-BLOCK_IDLE = 3
-TWO = 0
-HEAD = 0
-LATE = 14
-SMALL = 6
 RUN_BANKS = 8
-LAG = 8
-EDGE_LAG = 4
-VECTOR_EVERY = 6
-QLAG = 1
-TAIL = 1
-HEAD_RUN = 4
-FINISH = 2
+LAG_BANKS = 8
+LAST_LAG_BANKS = 4
 
+LOADS_AHEAD = 7
+RAW_BUFS = LOADS_AHEAD + 1
 PSUM_BANKS = 8
-RAW_BUFS = 8
-GROUPED_BUFS = (0, 3, 2)
-CODES_BUFS = (0, 5, 3)
+GROUPED_BUFS = {1: 3, 2: 2}
+CODES_BUFS = {1: 5, 2: 3}
+
+SMALL_LOADS_PIECE = 6
+SMALL_FLIPS_PIECE = 14
+
+IDLE_COLS = 512
+IDLE_BEFORE = 5
+IDLE_BLOCKS = 5
+IDLE_BEHIND = 3
 
 FLOPS = 2 * BATCH * FEATURES * NODES + 2 * BATCH * HIDDEN * OUTPUTS
+
+
+def flat(ap):
+    return ap.rearrange("p g r -> p (g r)")
 
 
 def tile_spn_k_kernel(tc, x, w0, w1, biases, out):
@@ -71,50 +82,44 @@ def tile_spn_k_kernel(tc, x, w0, w1, biases, out):
 
         rows_of = [w0[n * P : (n + 1) * P, :] for n in range(HIDDEN_BLOCKS)]
         rows_of += [x, w0[HIDDEN:NODES, :]]
-        items = []
-        for spec in PLAN:
-            if len(spec) == 3:
-                items.append((OUTPUT,) + spec[1:])
-            else:
-                items.extend((j,) + spec for j in (X, 0, 1, 2, 3))
-        hidden_end = max(m for m, item in enumerate(items) if item[0] < HIDDEN_BLOCKS)
 
-        blocks = [
-            (m, b) for m, item in enumerate(items) for b in range(rows_of[item[0]].shape[0] // P)
-        ]
+        pieces = []
+        for is_output, first, passes in ORDER:
+            if is_output:
+                pieces.append((OUTPUT, first, passes))
+            else:
+                pieces.extend((what, first, passes) for what in (X, 0, 1, 2, 3))
+        last_hidden = max(m for m, piece in enumerate(pieces) if piece[0] < HIDDEN_BLOCKS)
+
+        def row_blocks(what):
+            return rows_of[what].shape[0] // P
+
+        to_load = [(m, b) for m, piece in enumerate(pieces) for b in range(row_blocks(piece[0]))]
         raw_tiles = {}
-        taken = []
 
         def load_until(count):
-            for m, b in blocks[len(taken) : count]:
-                j, first, passes = items[m]
+            for m, b in to_load[len(raw_tiles) : count]:
+                what, first, passes = pieces[m]
                 raw = raws.tile([P, passes * K_PASS], BF16, align_bytes=MX_ALIGN)
                 cols = slice(first * K_PASS, (first + passes) * K_PASS)
-                rows = rows_of[j][b * P : (b + 1) * P, cols]
-                half = passes * K_PASS // 2
-                if TWO:
-                    nc.sync.dma_start(out=raw[:, 0:half], in_=rows[:, 0:half])
-                    nc.scalar.dma_start(out=raw[:, half : 2 * half], in_=rows[:, half : 2 * half])
-                else:
-                    nc.sync.dma_start(out=raw[:], in_=rows)
+                nc.sync.dma_start(out=raw[:], in_=rows_of[what][b * P : (b + 1) * P, cols])
                 raw_tiles[(m, b)] = raw
-                taken.append((m, b))
 
-        load_until(LOOK)
+        load_until(LOADS_AHEAD)
 
         bias_rows = consts.tile([P, P], BF16)
         nc.vector.memset(bias_rows[:], 0.0)
         idle_rows = consts.tile([P, IDLE_COLS], BF16)
         nc.vector.memset(idle_rows[:], 0.0)
 
-        def keep_busy(count):
+        def multiply_zeros(count):
             unread = psum.tile([P, IDLE_COLS], F32, tag="bank")
             for unused in range(count):
                 nc.tensor.matmul(
                     unread[:], lhsT=idle_rows[:, 0:P], rhs=idle_rows[:], start=True, stop=True
                 )
 
-        keep_busy(FIRST_IDLE)
+        multiply_zeros(IDLE_BEFORE)
         ident_f32 = consts.tile([P, P], F32)
         make_identity(nc, ident_f32[:])
         ident_bf16 = consts.tile([P, P], BF16)
@@ -128,20 +133,23 @@ def tile_spn_k_kernel(tc, x, w0, w1, biases, out):
         w1_scales = consts.tile([P, OUTPUTS], U8, align_bytes=MX_ALIGN)
         x_codes = consts.tile([P, PASSES, BATCH], U32, align_bytes=MX_ALIGN)
         x_scales = consts.tile([P, PASSES, BATCH], U8, align_bytes=MX_ALIGN)
-        hidden_acc = consts.tile([P, HIDDEN_BLOCKS, BATCH], F32)
-        out_acc = consts.tile([P, PAIR, OUTPUTS], F32)
+        hidden_total = consts.tile([P, HIDDEN_BLOCKS, BATCH], F32)
+        out_total = consts.tile([P, PAIR, OUTPUTS], F32)
         h_planes = consts.tile([P, PACK, BATCH], BF16)
         h_grouped = consts.tile([P, BATCH, PACK], BF16, align_bytes=MX_ALIGN)
         h_codes = consts.tile([P, BATCH], U32, align_bytes=MX_ALIGN)
         h_scales = consts.tile([P, BATCH], U8, align_bytes=MX_ALIGN)
 
-        def load_small():
-            nc.sync.dma_start(out=w1_raw[:], in_=w1.rearrange("(j p) k -> p j k", p=P))
+        def quantise(grouped, codes, scales):
+            nc.vector.quantize_mx(out=codes.bitcast(FP8X4), scales=scales, in_=grouped)
+
+        def load_biases_and_w1():
+            nc.sync.dma_start(out=w1_raw[:], in_=w1.rearrange("(b p) k -> p b k", p=P))
             nc.sync.dma_start(
                 out=bias_rows[0 : NODES // P, :], in_=biases.rearrange("(n p) -> n p", p=P)
             )
 
-        def spread_bias():
+        def stage_biases():
             flipped = psum.tile([P, P], BF16, tag="bank")
             nc.tensor.transpose(flipped[:], bias_rows[:], ident_bf16[:])
             nc.vector.tensor_copy(out=bias_cols[:], in_=flipped[:, 0:HIDDEN_BLOCKS])
@@ -158,13 +166,10 @@ def tile_spn_k_kernel(tc, x, w0, w1, biases, out):
             nc.vector.tensor_copy(out=out_bias[:], in_=chosen[:])
             for b in range(PAIR):
                 nc.vector.tensor_tensor(
-                    out=out_acc[:, b, :], in0=out_acc[:, b, :], in1=out_bias[:], op=ALU.add
+                    out=out_total[:, b, :], in0=out_total[:, b, :], in1=out_bias[:], op=ALU.add
                 )
 
-        def quantise(grouped, codes, scales):
-            nc.vector.quantize_mx(out=codes.bitcast(FP8X4), scales=scales, in_=grouped)
-
-        def flip_w1():
+        def stage_w1():
             flipped = psum.tile([P, PAIR, PACK, P], BF16, tag="bank")
             for b in range(PAIR):
                 for t in range(PACK):
@@ -172,8 +177,9 @@ def tile_spn_k_kernel(tc, x, w0, w1, biases, out):
                         flipped[:, b, t, :], w1_raw[:, b, t * P : (t + 1) * P], ident_bf16[:]
                     )
             nc.scalar.copy(out=w1_grouped[:], in_=flipped[:].rearrange("p b t o -> p b o t"))
+            quantise(w1_grouped[:].rearrange("p b o t -> p (b o t)"), w1_codes[:], w1_scales[:])
 
-        banks_done = []
+        banks_flipped = []
         due_quants = []
 
         def quantise_due(left):
@@ -182,17 +188,15 @@ def tile_spn_k_kernel(tc, x, w0, w1, biases, out):
                 quantise(*args)
             due_quants[:] = due_quants[count:]
 
-        def flat(ap):
-            return ap.rearrange("p g r -> p (g r)")
-
         def flip(raw, b, blocks, grouped, codes, scales):
             passes = codes.shape[1]
             raw_words = raw[:].bitcast(F32)
             words = grouped[:].bitcast(F32).rearrange(
                 "p (g b r u) -> p g b r u", g=passes, b=blocks, u=WORDS
             )
+            quant_passes = QUANT_COLS // (BLOCK_COLS * blocks)
             for g in range(0, passes, BANK_PASSES):
-                span = slice(g, g + BANK_PASSES)
+                end = g + BANK_PASSES
                 flipped = psum.tile([P, BANK_PASSES, WORDS, P], F32, tag="bank")
                 for i in range(BANK_PASSES):
                     for u in range(WORDS):
@@ -201,37 +205,38 @@ def tile_spn_k_kernel(tc, x, w0, w1, biases, out):
                             flipped[:, i, u, :], raw_words[:, word : word + P], ident_f32[:]
                         )
                 source = flipped[:].rearrange("p i u r -> p i r u")
-                if len(banks_done) % VECTOR_EVERY == 2:
-                    nc.vector.tensor_copy(out=words[:, span, b], in_=source)
+                if blocks == 1 and g == BANK_PASSES:
+                    nc.vector.tensor_copy(out=words[:, g:end, b], in_=source)
                 else:
-                    nc.scalar.copy(out=words[:, span, b], in_=source)
-                banks_done.append(g)
-                quant_passes = 2 * PAIR // blocks
-                if b == blocks - 1 and (g + BANK_PASSES) % quant_passes == 0:
-                    start = g + BANK_PASSES - quant_passes
-                    span = slice(start, start + quant_passes)
-                    cols = slice(start * BANK_COLS * blocks, (start + quant_passes) * BANK_COLS * blocks)
+                    nc.scalar.copy(out=words[:, g:end, b], in_=source)
+                banks_flipped.append(g)
+                if b == blocks - 1 and end % quant_passes == 0:
+                    span = slice(end - quant_passes, end)
+                    cols = slice(span.start * BLOCK_COLS * blocks, end * BLOCK_COLS * blocks)
                     due_quants.append((
                         grouped[:, cols], flat(codes[:, span, :]), flat(scales[:, span, :])
                     ))
-                quantise_due(QLAG)
+                quantise_due(1)
 
         due_products = []
-        due_adds = []
-        open_sums = {}
+        due_sums = []
+        due_relus = []
+        sums_of = {}
 
-        def sums_key(item):
-            return (item[0] // PAIR, item[1])
+        def sums_key(piece):
+            return (piece[0] // PAIR, piece[1])
 
-        def product(item, codes, scales, b, g):
-            j, first, passes = item
-            sums = open_sums[sums_key(item)][:, b if j == OUTPUT else j % PAIR, :]
+        def product(piece, codes, scales, b, g):
+            what, first, passes = piece
+            is_output = what == OUTPUT
+            half = b if is_output else what % PAIR
+            sums = sums_of[sums_key(piece)][:, half, :]
             rows = slice(b * P, (b + 1) * P)
             x_side = (x_codes[:, first + g, :], x_scales[:, first + g, :])
             w_side = (codes[:, g, :], scales[:, g, :])
-            still, moving = (x_side, w_side) if j == OUTPUT else (w_side, x_side)
+            still, moving = (x_side, w_side) if is_output else (w_side, x_side)
             last = g == passes - 1
-            with_h = j == OUTPUT and first + passes == PASSES
+            with_h = is_output and first + passes == PASSES
             nc.tensor.matmul_mx(
                 out=sums,
                 lhsT=still[0][:, rows].bitcast(FP8X4),
@@ -251,41 +256,27 @@ def tile_spn_k_kernel(tc, x, w0, w1, biases, out):
                     start=False,
                     stop=True,
                 )
-            if last and (b == PAIR - 1 or j in (1, 3)):
-                due_adds.append(item)
+            if last and half == PAIR - 1:
+                due_sums.append(piece)
 
         def multiply(lag):
-            ready = [args for args in due_products if len(banks_done) - args[-1] >= lag]
-            for item, codes, scales, b, g, staged in ready:
-                if sums_key(item) not in open_sums:
-                    sums = psum.tile([P, PAIR, PAIR_ROWS], F32, tag="bank")
-                    open_sums[sums_key(item)] = sums
-                product(item, codes, scales, b, g)
+            ready = [args for args in due_products if len(banks_flipped) - args[-1] >= lag]
+            for piece, codes, scales, b, g, flipped_then in ready:
+                if sums_key(piece) not in sums_of:
+                    sums = psum.tile([P, PAIR, BATCH], F32, tag="bank")
+                    sums_of[sums_key(piece)] = sums
+                product(piece, codes, scales, b, g)
             due_products[:] = due_products[len(ready):]
 
-        due_relus = []
-
-        def relu_due():
-            for n in due_relus:
-                for block in range(n, n + PAIR):
-                    nc.vector.tensor_scalar(
-                        out=h_planes[:, block, :],
-                        in0=hidden_acc[:, block, :],
-                        scalar1=bias_cols[:, block : block + 1],
-                        scalar2=0.0,
-                        op0=ALU.add,
-                        op1=ALU.max,
-                    )
-            due_relus.clear()
-
-        def add_due():
-            for item in due_adds:
-                j, first, passes = item
-                sums = open_sums[sums_key(item)]
+        def add_sums():
+            for piece in due_sums:
+                what, first, passes = piece
+                sums = sums_of[sums_key(piece)]
                 begins, ends = first == 0, first + passes == PASSES
-                if j == OUTPUT:
+                if what == OUTPUT:
                     for b in range(PAIR):
-                        dest = out_acc[:, b, :]
+                        total = out_total[:, b, :]
+                        dest = total
                         if ends:
                             result = consts.tile([P, OUTPUTS], F32, name="result%d" % b)
                             dest = result[:]
@@ -293,74 +284,88 @@ def tile_spn_k_kernel(tc, x, w0, w1, biases, out):
                             nc.scalar.copy(out=dest, in_=sums[:, b, :])
                         else:
                             nc.vector.tensor_tensor(
-                                out=dest, in0=sums[:, b, :], in1=out_acc[:, b, :], op=ALU.add
+                                out=dest, in0=sums[:, b, :], in1=total, op=ALU.add
                             )
                         if ends:
                             queue = nc.sync if b == 0 else nc.scalar
                             queue.dma_start(out=out[b * P : (b + 1) * P, :], in_=dest)
                 else:
-                    n = j - 1
-                    acc = hidden_acc[:, n : n + PAIR, :]
+                    n = what + 1 - PAIR
+                    total = hidden_total[:, n : n + PAIR, :]
                     if begins:
-                        nc.scalar.copy(out=acc, in_=sums[:])
+                        nc.scalar.copy(out=total, in_=sums[:])
                     else:
-                        nc.vector.tensor_tensor(out=acc, in0=sums[:], in1=acc, op=ALU.add)
+                        nc.vector.tensor_tensor(out=total, in0=sums[:], in1=total, op=ALU.add)
                     if ends:
                         due_relus.append(n)
-            due_adds.clear()
+            due_sums.clear()
 
-        def finish_h():
+        def relu_due():
+            for n in due_relus:
+                for block in range(n, n + PAIR):
+                    nc.vector.tensor_scalar(
+                        out=h_planes[:, block, :],
+                        in0=hidden_total[:, block, :],
+                        scalar1=bias_cols[:, block : block + 1],
+                        scalar2=0.0,
+                        op0=ALU.add,
+                        op1=ALU.max,
+                    )
+            due_relus.clear()
+
+        def quantise_h():
             nc.vector.tensor_copy(out=h_grouped[:], in_=h_planes[:].rearrange("p t r -> p r t"))
             quantise(h_grouped[:].rearrange("p r t -> p (r t)"), h_codes[:], h_scales[:])
 
-        flushed = 0
-        done = []
-        for m, item in enumerate(items):
-            j, first, passes = item
-            count = rows_of[j].shape[0] // P
-            if m == SMALL:
-                load_small()
-            if j == X:
+        blocks_flipped = 0
+        banks_at_last_run = 0
+        for m, piece in enumerate(pieces):
+            what, first, passes = piece
+            blocks = row_blocks(what)
+            if m == SMALL_LOADS_PIECE:
+                load_biases_and_w1()
+            if what == X:
                 codes = x_codes[:, first : first + passes, :]
                 scales = x_scales[:, first : first + passes, :]
             else:
-                width = count * P
-                bufs = CODES_BUFS[count]
-                codes_tile = coded.tile([P, passes, width], U32, align_bytes=MX_ALIGN, tag="codes%d" % width, bufs=bufs)
-                scales_tile = coded.tile([P, passes, width], U8, align_bytes=MX_ALIGN, tag="scales%d" % width, bufs=bufs)
+                bufs = CODES_BUFS[blocks]
+                codes_tile = coded.tile(
+                    [P, passes, blocks * P], U32, align_bytes=MX_ALIGN,
+                    tag="codes%d" % blocks, bufs=bufs,
+                )
+                scales_tile = coded.tile(
+                    [P, passes, blocks * P], U8, align_bytes=MX_ALIGN,
+                    tag="scales%d" % blocks, bufs=bufs,
+                )
                 codes, scales = codes_tile[:], scales_tile[:]
             grouped = groups.tile(
-                [P, passes * BANK_COLS * count], BF16, align_bytes=MX_ALIGN,
-                tag="words%d" % count, bufs=GROUPED_BUFS[count],
+                [P, passes * BLOCK_COLS * blocks], BF16, align_bytes=MX_ALIGN,
+                tag="grouped%d" % blocks, bufs=GROUPED_BUFS[blocks],
             )
-            for b in range(count):
-                flip(raw_tiles[(m, b)], b, count, grouped, codes, scales)
-                done.append(b)
-                if len(done) <= IDLE_BLOCKS:
-                    keep_busy(BLOCK_IDLE)
-                load_until(len(done) + LOOK)
+            for b in range(blocks):
+                flip(raw_tiles[(m, b)], b, blocks, grouped, codes, scales)
+                blocks_flipped += 1
+                if blocks_flipped <= IDLE_BLOCKS:
+                    multiply_zeros(IDLE_BEHIND)
+                load_until(blocks_flipped + LOADS_AHEAD)
                 if b == 0:
-                    add_due()
+                    add_sums()
                     relu_due()
-            if m == LATE:
-                spread_bias()
-            if m == LATE:
-                flip_w1()
-            if m == LATE:
-                quantise(w1_grouped[:].rearrange("p b o t -> p (b o t)"), w1_codes[:], w1_scales[:])
-            run = HEAD_RUN if m < HEAD else RUN_BANKS
-            edge = m >= len(items) - TAIL
-            if len(banks_done) - flushed >= run or edge:
-                multiply(EDGE_LAG if edge else LAG)
-                flushed = len(banks_done)
-            if m == hidden_end + FINISH:
-                add_due()
+            if m == SMALL_FLIPS_PIECE:
+                stage_biases()
+                stage_w1()
+            is_last = m == len(pieces) - 1
+            if is_last or len(banks_flipped) - banks_at_last_run >= RUN_BANKS:
+                multiply(LAST_LAG_BANKS if is_last else LAG_BANKS)
+                banks_at_last_run = len(banks_flipped)
+            if m == last_hidden + 2:
+                add_sums()
                 relu_due()
-                finish_h()
-            if j != X:
-                for b in range(PAIR if j == OUTPUT else 1):
+                quantise_h()
+            if what != X:
+                for b in range(PAIR if what == OUTPUT else 1):
                     for g in range(passes):
-                        due_products.append((item, codes, scales, b, g, len(banks_done)))
+                        due_products.append((piece, codes, scales, b, g, len(banks_flipped)))
         quantise_due(0)
         multiply(0)
-        add_due()
+        add_sums()

from contextlib import ExitStack

import concourse.mybir as mybir
from concourse.masks import make_identity

F32 = mybir.dt.float32
BF16 = mybir.dt.bfloat16
U32 = mybir.dt.uint32
U8 = mybir.dt.uint8
FP8X4 = mybir.dt.float8_e4m3fn_x4
ALU = mybir.AluOpType

P = 128
PACK = 4
K_PASS = P * PACK
WORDS = PACK // 2
MX_ALIGN = 256

BATCH = 256
FEATURES = 16384
NODES = 768
HIDDEN = 512
OUTPUTS = NODES - HIDDEN

PAIR = 2
HIDDEN_BLOCKS = HIDDEN // P
PASSES = FEATURES // K_PASS

X = HIDDEN_BLOCKS
OUTPUT = HIDDEN_BLOCKS + 1

ORDER = (
    (False, 0, 8),
    (True, 0, 8),
    (False, 8, 8),
    (True, 8, 8),
    (False, 16, 8),
    (False, 24, 8),
    (True, 16, 8),
    (True, 24, 4),
    (True, 28, 4),
)

BANK_PASSES = 2
BLOCK_COLS = P * PACK
QUANT_COLS = 2048

RUN_BANKS = 8
LAG_BANKS = 8
LAST_LAG_BANKS = 4

LOADS_AHEAD = 7
RAW_BUFS = LOADS_AHEAD + 1
PSUM_BANKS = 8
GROUPED_BUFS = {1: 3, 2: 2}
CODES_BUFS = {1: 5, 2: 3}

SMALL_LOADS_PIECE = 6
SMALL_FLIPS_PIECE = 14

IDLE_COLS = 512
IDLE_BEFORE = 5
IDLE_BLOCKS = 5
IDLE_BEHIND = 3

FLOPS = 2 * BATCH * FEATURES * NODES + 2 * BATCH * HIDDEN * OUTPUTS


def flat(ap):
    return ap.rearrange("p g r -> p (g r)")


def tile_spn_k_kernel(tc, x, w0, w1, biases, out):
    nc = tc.nc
    with ExitStack() as ctx:
        ctx.enter_context(tc.manual_schedule())
        consts = ctx.enter_context(tc.tile_pool(name="consts", bufs=1))
        raws = ctx.enter_context(tc.tile_pool(name="raws", bufs=RAW_BUFS))
        groups = ctx.enter_context(tc.tile_pool(name="groups", bufs=1))
        coded = ctx.enter_context(tc.tile_pool(name="coded", bufs=1))
        psum = ctx.enter_context(tc.psum_pool(name="psum", bufs=PSUM_BANKS))

        rows_of = [w0[n * P : (n + 1) * P, :] for n in range(HIDDEN_BLOCKS)]
        rows_of += [x, w0[HIDDEN:NODES, :]]

        pieces = []
        for is_output, first, passes in ORDER:
            if is_output:
                pieces.append((OUTPUT, first, passes))
            else:
                pieces.extend((what, first, passes) for what in (X, 0, 1, 2, 3))
        last_hidden = max(m for m, piece in enumerate(pieces) if piece[0] < HIDDEN_BLOCKS)

        def row_blocks(what):
            return rows_of[what].shape[0] // P

        to_load = [(m, b) for m, piece in enumerate(pieces) for b in range(row_blocks(piece[0]))]
        raw_tiles = {}

        def load_until(count):
            for m, b in to_load[len(raw_tiles) : count]:
                what, first, passes = pieces[m]
                raw = raws.tile([P, passes * K_PASS], BF16, align_bytes=MX_ALIGN)
                cols = slice(first * K_PASS, (first + passes) * K_PASS)
                nc.sync.dma_start(out=raw[:], in_=rows_of[what][b * P : (b + 1) * P, cols])
                raw_tiles[(m, b)] = raw

        load_until(LOADS_AHEAD)

        bias_rows = consts.tile([P, P], BF16)
        nc.vector.memset(bias_rows[:], 0.0)
        idle_rows = consts.tile([P, IDLE_COLS], BF16)
        nc.vector.memset(idle_rows[:], 0.0)

        def multiply_zeros(count):
            unread = psum.tile([P, IDLE_COLS], F32, tag="bank")
            for unused in range(count):
                nc.tensor.matmul(
                    unread[:], lhsT=idle_rows[:, 0:P], rhs=idle_rows[:], start=True, stop=True
                )

        multiply_zeros(IDLE_BEFORE)
        ident_f32 = consts.tile([P, P], F32)
        make_identity(nc, ident_f32[:])
        ident_bf16 = consts.tile([P, P], BF16)
        make_identity(nc, ident_bf16[:])
        bias_cols = consts.tile([P, HIDDEN_BLOCKS], F32)
        out_bias = consts.tile([P, OUTPUTS], F32)

        w1_raw = consts.tile([P, PAIR, HIDDEN], BF16)
        w1_grouped = consts.tile([P, PAIR, P, PACK], BF16, align_bytes=MX_ALIGN)
        w1_codes = consts.tile([P, OUTPUTS], U32, align_bytes=MX_ALIGN)
        w1_scales = consts.tile([P, OUTPUTS], U8, align_bytes=MX_ALIGN)
        x_codes = consts.tile([P, PASSES, BATCH], U32, align_bytes=MX_ALIGN)
        x_scales = consts.tile([P, PASSES, BATCH], U8, align_bytes=MX_ALIGN)
        hidden_total = consts.tile([P, HIDDEN_BLOCKS, BATCH], F32)
        out_total = consts.tile([P, PAIR, OUTPUTS], F32)
        h_planes = consts.tile([P, PACK, BATCH], BF16)
        h_grouped = consts.tile([P, BATCH, PACK], BF16, align_bytes=MX_ALIGN)
        h_codes = consts.tile([P, BATCH], U32, align_bytes=MX_ALIGN)
        h_scales = consts.tile([P, BATCH], U8, align_bytes=MX_ALIGN)

        def quantise(grouped, codes, scales):
            nc.vector.quantize_mx(out=codes.bitcast(FP8X4), scales=scales, in_=grouped)

        def load_biases_and_w1():
            nc.sync.dma_start(out=w1_raw[:], in_=w1.rearrange("(b p) k -> p b k", p=P))
            nc.sync.dma_start(
                out=bias_rows[0 : NODES // P, :], in_=biases.rearrange("(n p) -> n p", p=P)
            )

        def stage_biases():
            flipped = psum.tile([P, P], BF16, tag="bank")
            nc.tensor.transpose(flipped[:], bias_rows[:], ident_bf16[:])
            nc.vector.tensor_copy(out=bias_cols[:], in_=flipped[:, 0:HIDDEN_BLOCKS])
            chosen = psum.tile([P, OUTPUTS], F32, tag="bank")
            for b in range(PAIR):
                row = HIDDEN_BLOCKS + b
                nc.tensor.matmul(
                    chosen[:, b * P : (b + 1) * P],
                    lhsT=ident_bf16[:, row : row + 1].to_broadcast([P, P]),
                    rhs=bias_rows[:],
                    start=True,
                    stop=True,
                )
            nc.vector.tensor_copy(out=out_bias[:], in_=chosen[:])
            for b in range(PAIR):
                nc.vector.tensor_tensor(
                    out=out_total[:, b, :], in0=out_total[:, b, :], in1=out_bias[:], op=ALU.add
                )

        def stage_w1():
            flipped = psum.tile([P, PAIR, PACK, P], BF16, tag="bank")
            for b in range(PAIR):
                for t in range(PACK):
                    nc.tensor.transpose(
                        flipped[:, b, t, :], w1_raw[:, b, t * P : (t + 1) * P], ident_bf16[:]
                    )
            nc.scalar.copy(out=w1_grouped[:], in_=flipped[:].rearrange("p b t o -> p b o t"))
            quantise(w1_grouped[:].rearrange("p b o t -> p (b o t)"), w1_codes[:], w1_scales[:])

        banks_flipped = []
        due_quants = []

        def quantise_due(left):
            count = max(len(due_quants) - left, 0)
            for args in due_quants[:count]:
                quantise(*args)
            due_quants[:] = due_quants[count:]

        def flip(raw, b, blocks, grouped, codes, scales):
            passes = codes.shape[1]
            raw_words = raw[:].bitcast(F32)
            words = grouped[:].bitcast(F32).rearrange(
                "p (g b r u) -> p g b r u", g=passes, b=blocks, u=WORDS
            )
            quant_passes = QUANT_COLS // (BLOCK_COLS * blocks)
            for g in range(0, passes, BANK_PASSES):
                end = g + BANK_PASSES
                flipped = psum.tile([P, BANK_PASSES, WORDS, P], F32, tag="bank")
                for i in range(BANK_PASSES):
                    for u in range(WORDS):
                        word = ((g + i) * WORDS + u) * P
                        nc.tensor.transpose(
                            flipped[:, i, u, :], raw_words[:, word : word + P], ident_f32[:]
                        )
                source = flipped[:].rearrange("p i u r -> p i r u")
                if blocks == 1 and g == BANK_PASSES:
                    nc.vector.tensor_copy(out=words[:, g:end, b], in_=source)
                else:
                    nc.scalar.copy(out=words[:, g:end, b], in_=source)
                banks_flipped.append(g)
                if b == blocks - 1 and end % quant_passes == 0:
                    span = slice(end - quant_passes, end)
                    cols = slice(span.start * BLOCK_COLS * blocks, end * BLOCK_COLS * blocks)
                    due_quants.append((
                        grouped[:, cols], flat(codes[:, span, :]), flat(scales[:, span, :])
                    ))
                quantise_due(1)

        due_products = []
        due_sums = []
        due_relus = []
        sums_of = {}

        def sums_key(piece):
            return (piece[0] // PAIR, piece[1])

        def product(piece, codes, scales, b, g):
            what, first, passes = piece
            is_output = what == OUTPUT
            half = b if is_output else what % PAIR
            sums = sums_of[sums_key(piece)][:, half, :]
            rows = slice(b * P, (b + 1) * P)
            x_side = (x_codes[:, first + g, :], x_scales[:, first + g, :])
            w_side = (codes[:, g, :], scales[:, g, :])
            still, moving = (x_side, w_side) if is_output else (w_side, x_side)
            last = g == passes - 1
            with_h = is_output and first + passes == PASSES
            nc.tensor.matmul_mx(
                out=sums,
                lhsT=still[0][:, rows].bitcast(FP8X4),
                lhsT_scale=still[1][:, rows],
                rhs=moving[0].bitcast(FP8X4),
                rhs_scale=moving[1],
                start=(g == 0),
                stop=(last and not with_h),
            )
            if last and with_h:
                nc.tensor.matmul_mx(
                    out=sums,
                    lhsT=h_codes[:, rows].bitcast(FP8X4),
                    lhsT_scale=h_scales[:, rows],
                    rhs=w1_codes[:].bitcast(FP8X4),
                    rhs_scale=w1_scales[:],
                    start=False,
                    stop=True,
                )
            if last and half == PAIR - 1:
                due_sums.append(piece)

        def multiply(lag):
            ready = [args for args in due_products if len(banks_flipped) - args[-1] >= lag]
            for piece, codes, scales, b, g, flipped_then in ready:
                if sums_key(piece) not in sums_of:
                    sums = psum.tile([P, PAIR, BATCH], F32, tag="bank")
                    sums_of[sums_key(piece)] = sums
                product(piece, codes, scales, b, g)
            due_products[:] = due_products[len(ready):]

        def add_sums():
            for piece in due_sums:
                what, first, passes = piece
                sums = sums_of[sums_key(piece)]
                begins, ends = first == 0, first + passes == PASSES
                if what == OUTPUT:
                    for b in range(PAIR):
                        total = out_total[:, b, :]
                        dest = total
                        if ends:
                            result = consts.tile([P, OUTPUTS], F32, name="result%d" % b)
                            dest = result[:]
                        if begins:
                            nc.scalar.copy(out=dest, in_=sums[:, b, :])
                        else:
                            nc.vector.tensor_tensor(
                                out=dest, in0=sums[:, b, :], in1=total, op=ALU.add
                            )
                        if ends:
                            queue = nc.sync if b == 0 else nc.scalar
                            queue.dma_start(out=out[b * P : (b + 1) * P, :], in_=dest)
                else:
                    n = what + 1 - PAIR
                    total = hidden_total[:, n : n + PAIR, :]
                    if begins:
                        nc.scalar.copy(out=total, in_=sums[:])
                    else:
                        nc.vector.tensor_tensor(out=total, in0=sums[:], in1=total, op=ALU.add)
                    if ends:
                        due_relus.append(n)
            due_sums.clear()

        def relu_due():
            for n in due_relus:
                for block in range(n, n + PAIR):
                    nc.vector.tensor_scalar(
                        out=h_planes[:, block, :],
                        in0=hidden_total[:, block, :],
                        scalar1=bias_cols[:, block : block + 1],
                        scalar2=0.0,
                        op0=ALU.add,
                        op1=ALU.max,
                    )
            due_relus.clear()

        def quantise_h():
            nc.vector.tensor_copy(out=h_grouped[:], in_=h_planes[:].rearrange("p t r -> p r t"))
            quantise(h_grouped[:].rearrange("p r t -> p (r t)"), h_codes[:], h_scales[:])

        blocks_flipped = 0
        banks_at_last_run = 0
        for m, piece in enumerate(pieces):
            what, first, passes = piece
            blocks = row_blocks(what)
            if m == SMALL_LOADS_PIECE:
                load_biases_and_w1()
            if what == X:
                codes = x_codes[:, first : first + passes, :]
                scales = x_scales[:, first : first + passes, :]
            else:
                bufs = CODES_BUFS[blocks]
                codes_tile = coded.tile(
                    [P, passes, blocks * P], U32, align_bytes=MX_ALIGN,
                    tag="codes%d" % blocks, bufs=bufs,
                )
                scales_tile = coded.tile(
                    [P, passes, blocks * P], U8, align_bytes=MX_ALIGN,
                    tag="scales%d" % blocks, bufs=bufs,
                )
                codes, scales = codes_tile[:], scales_tile[:]
            grouped = groups.tile(
                [P, passes * BLOCK_COLS * blocks], BF16, align_bytes=MX_ALIGN,
                tag="grouped%d" % blocks, bufs=GROUPED_BUFS[blocks],
            )
            for b in range(blocks):
                flip(raw_tiles[(m, b)], b, blocks, grouped, codes, scales)
                blocks_flipped += 1
                if blocks_flipped <= IDLE_BLOCKS:
                    multiply_zeros(IDLE_BEHIND)
                load_until(blocks_flipped + LOADS_AHEAD)
                if b == 0:
                    add_sums()
                    relu_due()
            if m == SMALL_FLIPS_PIECE:
                stage_biases()
                stage_w1()
            is_last = m == len(pieces) - 1
            if is_last or len(banks_flipped) - banks_at_last_run >= RUN_BANKS:
                multiply(LAST_LAG_BANKS if is_last else LAG_BANKS)
                banks_at_last_run = len(banks_flipped)
            if m == last_hidden + 2:
                add_sums()
                relu_due()
                quantise_h()
            if what != X:
                for b in range(PAIR if what == OUTPUT else 1):
                    for g in range(passes):
                        due_products.append((piece, codes, scales, b, g, len(banks_flipped)))
        quantise_due(0)
        multiply(0)
        add_sums()
